import numpy as np
import ml_dtypes


def mxq(x, axis, fmt="e4m3"):
    dtype, down = {"e4m3": (ml_dtypes.float8_e4m3fn, 7), "e5m2": (ml_dtypes.float8_e5m2, 14)}[fmt]
    v = np.moveaxis(np.asarray(x, np.float32).astype(ml_dtypes.bfloat16).astype(np.float64), axis, -1)
    blocks = v.reshape(v.shape[:-1] + (-1, 32))
    amax = np.abs(blocks).max(-1, keepdims=True)
    byte = np.maximum(np.where(amax > 0, np.frexp(amax)[1] - 1 + 127, 0) - down, 1)
    scale = np.exp2(byte - 127.0)
    codes = (blocks / scale).astype(np.float32).astype(dtype).astype(np.float64)
    return np.moveaxis((codes * scale).reshape(v.shape), -1, axis)


WIDE = False


def mx_kscale(k):
    if not WIDE:
        return np.ones(k)
    levels = np.array([30, -30])
    if k % 512:
        return np.exp2(np.random.permutation(np.resize(levels, k // 32))).repeat(32)
    a = np.empty((k // 512, 16))
    for p in range(k // 512):
        a[p, :8] = np.random.permutation(np.resize(levels, 8))
        for g in range(8):
            far = levels[np.abs(levels - a[p, g]) >= 10]
            a[p, g + 8] = far[np.random.randint(len(far))]
    return np.exp2(a.ravel()).repeat(32)


BF16 = ml_dtypes.bfloat16


def bf(x):
    return np.asarray(x, np.float32).astype(BF16)


def f64(x):
    return np.asarray(x).astype(np.float64)


B, T, C, E = 4, 512, 1024, 1024
THETA = 10000.0


def rope_rotate(v):
    inv_freq = 1.0 / (THETA ** (f64(np.arange(0, E, 2)) / E))
    freqs = f64(np.arange(T))[:, None] * inv_freq[None, :]
    freqs = np.repeat(freqs, 2, axis=-1)
    cos, sin = np.cos(freqs), np.sin(freqs)
    vp = v.reshape(v.shape[:-1] + (E // 2, 2))
    v_rot = np.stack((-vp[..., 1], vp[..., 0]), axis=-1).reshape(v.shape)
    return v * cos + v_rot * sin


def setup_inputs():
    s = mx_kscale(C)
    return {
        "x": bf(np.random.standard_normal((B, T, C)) * s),
        "Wq": bf(np.random.standard_normal((C, E)) * 0.7 / np.sqrt(C) / s[:, None]),
        "bq": bf(np.random.standard_normal(E) * 0.2),
        "Wk": bf(np.random.standard_normal((C, E)) * 0.7 / np.sqrt(C) / s[:, None]),
        "bk": bf(np.random.standard_normal(E) * 0.2),
    }


def reference(x, Wq, bq, Wk, bk):
    xq = mxq(f64(x), 2, "e5m2")
    Q = rope_rotate((xq @ mxq(f64(Wq), 0, "e4m3")) + f64(bq))
    K = rope_rotate((xq @ mxq(f64(Wk), 0, "e4m3")) + f64(bk))
    return Q, K

@@ -1,0 +1,339 @@
+import math
+from contextlib import ExitStack
+
+import concourse.mybir as mybir
+from concourse.masks import make_identity
+
+B, T, C, E = 4, 512, 1024, 1024
+THETA = 10000.0
+FLOPS = 2 * 2 * B * T * C * E
+
+F32 = mybir.dt.float32
+BF16 = mybir.dt.bfloat16
+I32 = mybir.dt.int32
+U32 = mybir.dt.uint32
+U8 = mybir.dt.uint8
+E4M3 = mybir.dt.float8_e4m3fn_x4
+E5M2 = mybir.dt.float8_e5m2_x4
+ALU = mybir.AluOpType
+ACT = mybir.ActivationFunctionType
+
+P = 128
+PACK = 4
+K_PASS = P * PACK
+PASSES = C // K_PASS
+TOKEN_TILES = T // P
+PAIR_TILES = E // (2 * P)
+PROJ = 2
+UNITS_PER_PHASE = B * PROJ
+UNITS = PAIR_TILES * UNITS_PER_PHASE
+PARTITION_BITS = 7
+TWO_PI = 2.0 * math.pi
+
+
+def tile_attention_pa_kernel(tc, x, Wq, bq, Wk, bk, out_0, out_1):
+    nc = tc.nc
+    weights = (Wq, Wk)
+    biases = (bq, bk)
+    outs = (out_0, out_1)
+
+    def pair_tile(phase):
+        return PAIR_TILES - 1 - phase
+
+    def unit_coords(u):
+        phase, rest = divmod(u, UNITS_PER_PHASE)
+        b, proj = divmod(rest, PROJ)
+        return phase, b, proj
+
+    def summed_on_tensor(u):
+        return u % 4 == 3 or u >= UNITS - 2
+
+    with ExitStack() as ctx:
+        keep = ctx.enter_context(tc.tile_pool(name="keep", bufs=1))
+        work = ctx.enter_context(tc.tile_pool(name="work", bufs=2))
+        psum = ctx.enter_context(tc.psum_pool(name="psum", bufs=4))
+        ctx.enter_context(tc.manual_schedule())
+
+        x_raw, w_raw, bias_sb = {}, {}, {}
+        x_grouped, x_codes, x_scales = {}, {}, {}
+        w_grouped, w_codes, w_scales = {}, {}, {}
+        turns, tables = {}, {}
+        banks, products, sums = {}, {}, {}
+
+        def load_x(b, tt):
+            tile = keep.tile([P, C], BF16, name="x_raw_%d_%d" % (b, tt))
+            nc.sync.dma_start(out=tile[:], in_=x[b, tt * P : (tt + 1) * P, :])
+            x_raw[b, tt] = tile
+
+        def load_w(phase, proj, g):
+            j = pair_tile(phase)
+            tile = work.tile([P, PACK, 2 * P], BF16, name="w_raw", bufs=8)
+            rows = weights[proj][g * K_PASS : (g + 1) * K_PASS, j * 2 * P : (j + 1) * 2 * P]
+            nc.sync.dma_start(out=tile[:], in_=rows.rearrange("(p r) c -> p r c", r=PACK))
+            w_raw[phase, proj, g] = tile
+
+        def load_bias(proj):
+            tile = keep.tile([P, PAIR_TILES, 2], BF16, name="bias_%d" % proj)
+            nc.scalar.dma_start(out=tile[:], in_=biases[proj].rearrange("(j p h) -> p j h", p=P, h=2))
+            bias_sb[proj] = tile
+
+        def transpose_x(b, tt, copy):
+            if tt == 0:
+                x_grouped[b] = work.tile([P, PASSES, T * PACK], BF16, name="x_grouped", bufs=3, align_bytes=64)
+                x_codes[b] = keep.tile([P, PASSES, T], U32, name="x_codes_%d" % b, align_bytes=64)
+                x_scales[b] = keep.tile([P, PASSES, T], U8, name="x_scales_%d" % b, align_bytes=64)
+            words = x_raw[b, tt][:].bitcast(F32)
+            bank = psum.tile([P, PASSES, 2, P], F32, name="turn_bank")
+            for g in range(PASSES):
+                for half in range(2):
+                    nc.tensor.transpose(
+                        bank[:, g, half, :], words[:, 256 * g + half : 256 * (g + 1) : 2], identity[:]
+                    )
+            target = x_grouped[b][:, :, tt * P * PACK : (tt + 1) * P * PACK].bitcast(F32)
+            copy(
+                out=target.rearrange("p g (n u) -> p g n u", u=2),
+                in_=bank[:].rearrange("p g u n -> p g n u"),
+            )
+
+        def quantize_x(b, g, first, count):
+            nc.vector.quantize_mx(
+                out=x_codes[b][:, g, first : first + count].bitcast(E5M2),
+                scales=x_scales[b][:, g, first : first + count],
+                in_=x_grouped[b][:, g, first * PACK : (first + count) * PACK],
+            )
+
+        def interleave_w(phase, proj, g, copy):
+            if g == 0:
+                w_grouped[phase, proj] = work.tile(
+                    [P, PASSES, 2 * P * PACK], BF16, name="w_grouped", align_bytes=64
+                )
+            copy(
+                out=w_grouped[phase, proj][:, g, :].rearrange("p (h m r) -> p h m r", h=2, r=PACK),
+                in_=w_raw[phase, proj, g][:].rearrange("p r (m h) -> p h m r", h=2),
+            )
+
+        def quantize_w(phase, proj):
+            codes = work.tile([P, PASSES * 2 * P], U32, name="w_codes", bufs=4, align_bytes=64)
+            scales = work.tile([P, PASSES * 2 * P], U8, name="w_scales", bufs=4, align_bytes=64)
+            nc.vector.quantize_mx(
+                out=codes[:].bitcast(E4M3),
+                scales=scales[:],
+                in_=w_grouped[phase, proj][:].rearrange("p g n -> p (g n)"),
+            )
+            w_codes[phase, proj] = codes
+            w_scales[phase, proj] = scales
+
+        def needs_reduction(phase):
+            fastest = THETA ** (-pair_tile(phase) * P / (E // 2))
+            return (T - 1) * fastest > math.pi
+
+        def make_turns(phase):
+            j = pair_tile(phase)
+            tile = keep.tile([P, T], F32, name="turns_%d" % phase)
+            if needs_reduction(phase):
+                whole = work.tile([P, T], I32, name="whole_turns")
+                nc.vector.tensor_scalar(
+                    out=whole[:], in0=position[:], scalar1=rate[:, j : j + 1], scalar2=None, op0=ALU.mult
+                )
+                nc.vector.scalar_tensor_tensor(
+                    out=tile[:], in0=position[:], scalar=rate[:, j : j + 1], in1=whole[:],
+                    op0=ALU.mult, op1=ALU.subtract,
+                )
+            else:
+                nc.vector.tensor_scalar(
+                    out=tile[:], in0=position[:], scalar1=rate[:, j : j + 1], scalar2=None, op0=ALU.mult
+                )
+            turns[phase] = tile
+
+        def make_cos(phase):
+            tables[phase] = work.tile([P, 3, T], F32, name="table")
+            source = turns[phase]
+            if needs_reduction(phase):
+                source = work.tile([P, T], F32, name="magnitude")
+                nc.scalar.activation(out=source[:], in_=turns[phase][:], func=ACT.Abs)
+            nc.scalar.activation(
+                out=tables[phase][:, 1, :], in_=source[:], func=ACT.Sin, scale=-TWO_PI, bias=math.pi / 2
+            )
+
+        def make_sin(phase):
+            nc.scalar.activation(out=tables[phase][:, 2, :], in_=turns[phase][:], func=ACT.Sin, scale=TWO_PI)
+            nc.scalar.activation(out=tables[phase][:, 0, :], in_=turns[phase][:], func=ACT.Sin, scale=-TWO_PI)
+
+        def multiply(u):
+            phase, b, proj = unit_coords(u)
+            for h in range(2):
+                bank = psum.tile([P, T], F32, name="mx_bank")
+                for g in range(PASSES):
+                    cols = slice((2 * g + h) * P, (2 * g + h + 1) * P)
+                    nc.tensor.matmul_mx(
+                        out=bank[:],
+                        lhsT=w_codes[phase, proj][:, cols].bitcast(E4M3),
+                        lhsT_scale=w_scales[phase, proj][:, cols],
+                        rhs=x_codes[b][:, g, :].bitcast(E5M2),
+                        rhs_scale=x_scales[b][:, g, :],
+                        start=(g == 0),
+                        stop=(g == PASSES - 1),
+                    )
+                banks[u, h] = bank
+
+        def rotate(u):
+            phase, b, proj = unit_coords(u)
+            j = pair_tile(phase)
+            for h in range(2):
+                tile = work.tile([P, 2, T], F32, name="product", bufs=8)
+                nc.vector.scalar_tensor_tensor(
+                    out=tile[:],
+                    in0=banks[u, h][:].unsqueeze(1).to_broadcast([P, 2, T]),
+                    scalar=bias_sb[proj][:, j, h : h + 1],
+                    in1=tables[phase][:, 1 - h : 3 - h, :],
+                    op0=ALU.add,
+                    op1=ALU.mult,
+                )
+                products[u, h] = tile
+            if not summed_on_tensor(u):
+                total = work.tile([P, 2, T], F32, name="total", bufs=3)
+                nc.gpsimd.tensor_tensor(out=total[:], in0=products[u, 0][:], in1=products[u, 1][:], op=ALU.add)
+                sums[u] = total
+
+        def finish(u):
+            phase, b, proj = unit_coords(u)
+            j = pair_tile(phase)
+            terms = [products[u, 0], products[u, 1]] if summed_on_tensor(u) else [sums[u]]
+            last = u == UNITS - 1
+            rows = outs[proj][b, :, j * 2 * P : (j + 1) * 2 * P].rearrange("(t p) c -> p t c", p=P)
+            staged = work.tile([P, TOKEN_TILES, 2 * P], F32, name="staged", bufs=6)
+            for half in range(2):
+                bank = psum.tile([P, 2, 2, P], F32, name="turn_bank")
+                for k in range(2):
+                    tt = 2 * half + k
+                    for h in range(2):
+                        for i, term in enumerate(terms):
+                            nc.tensor.matmul(
+                                out=bank[:, k, h, :],
+                                lhsT=term[:, h, tt * P : (tt + 1) * P],
+                                rhs=identity[:],
+                                is_transpose=True,
+                                start=(i == 0),
+                                stop=(i == len(terms) - 1),
+                            )
+                tiles = slice(2 * half, 2 * half + 2)
+                copy = nc.vector.tensor_copy if last and half == 1 else nc.scalar.copy
+                copy(
+                    out=staged[:, tiles, :].rearrange("p t (i h) -> p t i h", h=2),
+                    in_=bank[:].rearrange("p t h i -> p t i h"),
+                )
+                if last:
+                    nc.sync.dma_start(out=rows[:, tiles, :], in_=staged[:, tiles, :])
+            if not last:
+                nc.sync.dma_start(out=rows, in_=staged[:])
+
+        for proj in range(PROJ):
+            load_bias(proj)
+        load_x(0, 0)
+        load_x(0, 1)
+        for g in range(PASSES):
+            load_w(0, 0, g)
+        load_x(0, 2)
+        load_x(0, 3)
+        for g in range(PASSES):
+            load_w(0, 1, g)
+        for tt in range(TOKEN_TILES):
+            load_x(1, tt)
+        load_w(1, 0, 0)
+        for b in range(2, B):
+            for tt in range(TOKEN_TILES):
+                load_x(b, tt)
+        load_w(1, 0, 1)
+        for g in range(PASSES):
+            load_w(1, 1, g)
+
+        index = keep.tile([P, PARTITION_BITS], I32)
+        nc.gpsimd.iota(index[:], pattern=[[0, PARTITION_BITS]], base=0, channel_multiplier=1)
+        shift = keep.tile([P, PARTITION_BITS], I32)
+        nc.gpsimd.iota(shift[:], pattern=[[1, PARTITION_BITS]], base=0, channel_multiplier=0)
+        identity = keep.tile([P, P], F32)
+        make_identity(nc, identity[:])
+        position = keep.tile([P, T], F32)
+        nc.gpsimd.iota(
+            position[:], pattern=[[1, T]], base=0, channel_multiplier=0, allow_small_or_imprecise_dtypes=True
+        )
+
+        shifted = keep.tile([P, PARTITION_BITS], I32)
+        nc.vector.tensor_tensor(out=shifted[:], in0=index[:], in1=shift[:], op=ALU.logical_shift_right)
+        bits = keep.tile([P, PARTITION_BITS], I32)
+        nc.vector.tensor_scalar(out=bits[:], in0=shifted[:], scalar1=1, scalar2=None, op0=ALU.bitwise_and)
+        factors = keep.tile([P, PARTITION_BITS], F32)
+        for bit in range(PARTITION_BITS):
+            ratio = THETA ** (-(2**bit) / (E // 2))
+            nc.vector.tensor_scalar(
+                out=factors[:, bit : bit + 1], in0=bits[:, bit : bit + 1],
+                scalar1=ratio - 1.0, scalar2=1.0, op0=ALU.mult, op1=ALU.add,
+            )
+        base_rate = keep.tile([P, 1], F32)
+        nc.vector.tensor_reduce(out=base_rate[:], in_=factors[:], axis=mybir.AxisListType.X, op=ALU.mult)
+        rate = keep.tile([P, PAIR_TILES], F32)
+        for j in range(PAIR_TILES):
+            nc.vector.tensor_scalar(
+                out=rate[:, j : j + 1], in0=base_rate[:],
+                scalar1=THETA ** (-j * P / (E // 2)) / TWO_PI, scalar2=None, op0=ALU.mult,
+            )
+
+        make_turns(0)
+        make_cos(0)
+        make_sin(0)
+        make_turns(1)
+
+        transpose_x(0, 0, nc.scalar.copy)
+        transpose_x(0, 1, nc.scalar.copy)
+        for g in range(PASSES):
+            interleave_w(0, 0, g, nc.vector.tensor_copy)
+        for g in range(PASSES):
+            quantize_x(0, g, 0, 2 * P)
+        quantize_w(0, 0)
+        transpose_x(0, 2, nc.scalar.copy)
+        transpose_x(0, 3, nc.scalar.copy)
+        make_turns(2)
+        for g in range(PASSES):
+            quantize_x(0, g, 2 * P, 2 * P)
+        multiply(0)
+        for g in range(PASSES):
+            interleave_w(0, 1, g, nc.vector.tensor_copy)
+        make_turns(3)
+        quantize_w(0, 1)
+        for tt in range(TOKEN_TILES):
+            transpose_x(1, tt, nc.scalar.copy)
+
+        for step in range(UNITS):
+            phase, offset = divmod(step, UNITS_PER_PHASE)
+            ahead = phase + 1
+            if step + 1 < UNITS:
+                multiply(step + 1)
+            if ahead < PAIR_TILES:
+                if offset == 0:
+                    make_cos(ahead)
+                if offset == 2:
+                    make_sin(ahead)
+                if offset == 1:
+                    interleave_w(ahead, 0, 0, nc.scalar.copy)
+                if offset == 5:
+                    interleave_w(ahead, 0, 1, nc.scalar.copy)
+                if offset == 6:
+                    interleave_w(ahead, 1, 0, nc.scalar.copy)
+                if offset == 7:
+                    interleave_w(ahead, 1, 1, nc.scalar.copy)
+            rotate(step)
+            b_turn, second = divmod(step + 4, 2)
+            if b_turn < B:
+                for tt in range(2 * second, 2 * second + 2):
+                    transpose_x(b_turn, tt, nc.scalar.copy)
+            if not second and b_turn - 1 < B:
+                for g in range(PASSES):
+                    quantize_x(b_turn - 1, g, 0, T)
+            if ahead < PAIR_TILES and offset >= 6:
+                quantize_w(ahead, offset - 6)
+            if step >= 2:
+                finish(step - 2)
+            if ahead + 1 < PAIR_TILES and offset >= 4:
+                load_w(ahead + 1, (offset - 4) // 2, offset % 2)
+        finish(UNITS - 2)
+        finish(UNITS - 1)

@@ -29,6 +29,15 @@ UNITS_PER_PHASE = B * PROJ
 UNITS = PAIR_TILES * UNITS_PER_PHASE
 PARTITION_BITS = 7
 TWO_PI = 2.0 * math.pi
+LOAD_AHEAD = 13
+QUANT_LEAD = 2
+PREP_LEAD = 5
+X1_BEFORE = 1
+X1_MID = 4
+TLEAD = 4
+XLEAD = 7
+FINE = 3
+TAIL_UNITS = 2
 
 
 def tile_attention_pa_kernel(tc, x, Wq, bq, Wk, bk, out_0, out_1):
@@ -40,13 +49,27 @@ def tile_attention_pa_kernel(tc, x, Wq, bq, Wk, bk, out_0, out_1):
     def pair_tile(phase):
         return PAIR_TILES - 1 - phase
 
+    order = [(0, 0)]
+    slabs, batches = 1, 1
+    while len(order) < UNITS:
+        if slabs == batches:
+            order += [(s, b) for s in range(slabs, 2 * slabs) for b in range(batches)]
+            slabs *= 2
+        else:
+            order += [(s, b) for b in range(batches, 2 * batches) for s in range(slabs)]
+            batches *= 2
+    first_slab = {s: min(u for u in range(UNITS) if order[u][0] == s) for s in range(slabs)}
+    first_batch = {b: min(u for u in range(UNITS) if order[u][1] == b) for b in range(batches)}
+    new_slab = {u: s for s, u in first_slab.items()}
+    new_batch = {u: b for b, u in first_batch.items()}
+
     def unit_coords(u):
-        phase, rest = divmod(u, UNITS_PER_PHASE)
-        b, proj = divmod(rest, PROJ)
+        slab, b = order[u]
+        phase, proj = divmod(slab, PROJ)
         return phase, b, proj
 
     def summed_on_tensor(u):
-        return u % 4 == 3 or u >= UNITS - 2
+        return u + QUANT_LEAD + 1 in new_slab or u + QUANT_LEAD + 1 in new_batch or u == 0 or u >= UNITS - TAIL_UNITS
 
     with ExitStack() as ctx:
         keep = ctx.enter_context(tc.tile_pool(name="keep", bufs=1))
@@ -112,52 +135,64 @@ def tile_attention_pa_kernel(tc, x, Wq, bq, Wk, bk, out_0, out_1):
                 in_=w_raw[phase, proj, g][:].rearrange("p r (m h) -> p h m r", h=2),
             )
 
-        def quantize_w(phase, proj):
-            codes = work.tile([P, PASSES * 2 * P], U32, name="w_codes", bufs=4, align_bytes=64)
-            scales = work.tile([P, PASSES * 2 * P], U8, name="w_scales", bufs=4, align_bytes=64)
+        def quantize_w(phase, proj, first=0, count=PASSES):
+            if first == 0:
+                w_codes[phase, proj] = work.tile([P, PASSES * 2 * P], U32, name="w_codes", bufs=8, align_bytes=64)
+                w_scales[phase, proj] = work.tile([P, PASSES * 2 * P], U8, name="w_scales", bufs=8, align_bytes=64)
+            cols = slice(first * 2 * P, (first + count) * 2 * P)
             nc.vector.quantize_mx(
-                out=codes[:].bitcast(E4M3),
-                scales=scales[:],
-                in_=w_grouped[phase, proj][:].rearrange("p g n -> p (g n)"),
+                out=w_codes[phase, proj][:, cols].bitcast(E4M3),
+                scales=w_scales[phase, proj][:, cols],
+                in_=w_grouped[phase, proj][:, first : first + count, :].rearrange("p g n -> p (g n)"),
             )
-            w_codes[phase, proj] = codes
-            w_scales[phase, proj] = scales
 
-        def needs_reduction(phase):
-            fastest = THETA ** (-pair_tile(phase) * P / (E // 2))
-            return (T - 1) * fastest > math.pi
+        def largest_angle(phase):
+            return (T - 1) * THETA ** (-pair_tile(phase) * P / (E // 2))
 
-        def make_turns(phase):
+        def reduce_turns(phase):
             j = pair_tile(phase)
+            whole = work.tile([P, T], I32, name="whole_turns")
+            nc.vector.tensor_scalar(
+                out=whole[:], in0=position[:], scalar1=rate[:, j, 0:1], scalar2=None, op0=ALU.mult
+            )
             tile = keep.tile([P, T], F32, name="turns_%d" % phase)
-            if needs_reduction(phase):
-                whole = work.tile([P, T], I32, name="whole_turns")
-                nc.vector.tensor_scalar(
-                    out=whole[:], in0=position[:], scalar1=rate[:, j : j + 1], scalar2=None, op0=ALU.mult
-                )
-                nc.vector.scalar_tensor_tensor(
-                    out=tile[:], in0=position[:], scalar=rate[:, j : j + 1], in1=whole[:],
-                    op0=ALU.mult, op1=ALU.subtract,
-                )
-            else:
-                nc.vector.tensor_scalar(
-                    out=tile[:], in0=position[:], scalar1=rate[:, j : j + 1], scalar2=None, op0=ALU.mult
-                )
+            nc.vector.scalar_tensor_tensor(
+                out=tile[:], in0=position[:], scalar=rate[:, j, 0:1], in1=whole[:],
+                op0=ALU.mult, op1=ALU.subtract,
+            )
             turns[phase] = tile
 
         def make_cos(phase):
-            tables[phase] = work.tile([P, 3, T], F32, name="table")
-            source = turns[phase]
-            if needs_reduction(phase):
-                source = work.tile([P, T], F32, name="magnitude")
-                nc.scalar.activation(out=source[:], in_=turns[phase][:], func=ACT.Abs)
-            nc.scalar.activation(
-                out=tables[phase][:, 1, :], in_=source[:], func=ACT.Sin, scale=-TWO_PI, bias=math.pi / 2
-            )
+            j = pair_tile(phase)
+            tables[phase] = work.tile([P, 3, T], F32, name="table", bufs=3)
+            plane = tables[phase][:, 1, :]
+            if largest_angle(phase) < math.pi / 2:
+                nc.scalar.activation(
+                    out=plane, in_=position[:], func=ACT.Sin, scale=rate[:, j, 0:1], bias=math.pi / 2
+                )
+                return
+            magnitude = work.tile([P, T], F32, name="magnitude")
+            if largest_angle(phase) < TWO_PI:
+                nc.scalar.activation(
+                    out=magnitude[:], in_=position[:], func=ACT.Abs, scale=rate[:, j, 0:1], bias=-math.pi
+                )
+                nc.scalar.activation(out=plane, in_=magnitude[:], func=ACT.Sin, bias=-math.pi / 2)
+            else:
+                nc.scalar.activation(out=magnitude[:], in_=turns[phase][:], func=ACT.Abs)
+                nc.scalar.activation(out=plane, in_=magnitude[:], func=ACT.Sin, scale=-TWO_PI, bias=math.pi / 2)
 
         def make_sin(phase):
-            nc.scalar.activation(out=tables[phase][:, 2, :], in_=turns[phase][:], func=ACT.Sin, scale=TWO_PI)
-            nc.scalar.activation(out=tables[phase][:, 0, :], in_=turns[phase][:], func=ACT.Sin, scale=-TWO_PI)
+            j = pair_tile(phase)
+            plus, minus = tables[phase][:, 2, :], tables[phase][:, 0, :]
+            if largest_angle(phase) < math.pi / 2:
+                nc.scalar.activation(out=plus, in_=position[:], func=ACT.Sin, scale=rate[:, j, 0:1])
+                nc.scalar.activation(out=minus, in_=position[:], func=ACT.Sin, scale=rate[:, j, 1:2])
+            elif largest_angle(phase) < TWO_PI:
+                nc.scalar.activation(out=plus, in_=position[:], func=ACT.Sin, scale=rate[:, j, 1:2], bias=math.pi)
+                nc.scalar.activation(out=minus, in_=position[:], func=ACT.Sin, scale=rate[:, j, 0:1], bias=-math.pi)
+            else:
+                nc.scalar.activation(out=plus, in_=turns[phase][:], func=ACT.Sin, scale=TWO_PI)
+                nc.scalar.activation(out=minus, in_=turns[phase][:], func=ACT.Sin, scale=-TWO_PI)
 
         def multiply(u):
             phase, b, proj = unit_coords(u)
@@ -176,76 +211,79 @@ def tile_attention_pa_kernel(tc, x, Wq, bq, Wk, bk, out_0, out_1):
                     )
                 banks[u, h] = bank
 
-        def rotate(u):
+        def rotate(u, h, first=0, count=T):
             phase, b, proj = unit_coords(u)
             j = pair_tile(phase)
-            for h in range(2):
-                tile = work.tile([P, 2, T], F32, name="product", bufs=8)
-                nc.vector.scalar_tensor_tensor(
-                    out=tile[:],
-                    in0=banks[u, h][:].unsqueeze(1).to_broadcast([P, 2, T]),
-                    scalar=bias_sb[proj][:, j, h : h + 1],
-                    in1=tables[phase][:, 1 - h : 3 - h, :],
-                    op0=ALU.add,
-                    op1=ALU.mult,
-                )
-                products[u, h] = tile
-            if not summed_on_tensor(u):
-                total = work.tile([P, 2, T], F32, name="total", bufs=3)
-                nc.gpsimd.tensor_tensor(out=total[:], in0=products[u, 0][:], in1=products[u, 1][:], op=ALU.add)
-                sums[u] = total
+            if first == 0:
+                products[u, h] = work.tile([P, 2, T], F32, name="product", bufs=8)
+            cols = slice(first, first + count)
+            nc.vector.scalar_tensor_tensor(
+                out=products[u, h][:, :, cols],
+                in0=banks[u, h][:, cols].unsqueeze(1).to_broadcast([P, 2, count]),
+                scalar=bias_sb[proj][:, j, h : h + 1],
+                in1=tables[phase][:, 1 - h : 3 - h, cols],
+                op0=ALU.add,
+                op1=ALU.mult,
+            )
+
+        def add_products(u):
+            total = work.tile([P, 2, T], F32, name="total", bufs=3)
+            nc.gpsimd.tensor_tensor(out=total[:], in0=products[u, 0][:], in1=products[u, 1][:], op=ALU.add)
+            sums[u] = total
+
+        def turn_back(u, half, staged, copy):
+            terms = [products[u, 0], products[u, 1]] if summed_on_tensor(u) else [sums[u]]
+            bank = psum.tile([P, 2, 2, P], F32, name="turn_bank")
+            for k in range(2):
+                tt = 2 * half + k
+                for h in range(2):
+                    for i, term in enumerate(terms):
+                        nc.tensor.matmul(
+                            out=bank[:, k, h, :],
+                            lhsT=term[:, h, tt * P : (tt + 1) * P],
+                            rhs=identity[:],
+                            is_transpose=True,
+                            start=(i == 0),
+                            stop=(i == len(terms) - 1),
+                        )
+            copy(
+                out=staged[:, 2 * half : 2 * half + 2, :].rearrange("p t (i h) -> p t i h", h=2),
+                in_=bank[:].rearrange("p t h i -> p t i h"),
+            )
+
+        def out_rows(u):
+            phase, b, proj = unit_coords(u)
+            j = pair_tile(phase)
+            return outs[proj][b, :, j * 2 * P : (j + 1) * 2 * P].rearrange("(t p) c -> p t c", p=P)
 
         def finish(u):
-            phase, b, proj = unit_coords(u)
-            j = pair_tile(phase)
-            terms = [products[u, 0], products[u, 1]] if summed_on_tensor(u) else [sums[u]]
-            last = u == UNITS - 1
-            rows = outs[proj][b, :, j * 2 * P : (j + 1) * 2 * P].rearrange("(t p) c -> p t c", p=P)
             staged = work.tile([P, TOKEN_TILES, 2 * P], F32, name="staged", bufs=6)
             for half in range(2):
-                bank = psum.tile([P, 2, 2, P], F32, name="turn_bank")
-                for k in range(2):
-                    tt = 2 * half + k
-                    for h in range(2):
-                        for i, term in enumerate(terms):
-                            nc.tensor.matmul(
-                                out=bank[:, k, h, :],
-                                lhsT=term[:, h, tt * P : (tt + 1) * P],
-                                rhs=identity[:],
-                                is_transpose=True,
-                                start=(i == 0),
-                                stop=(i == len(terms) - 1),
-                            )
-                tiles = slice(2 * half, 2 * half + 2)
-                copy = nc.vector.tensor_copy if last and half == 1 else nc.scalar.copy
-                copy(
-                    out=staged[:, tiles, :].rearrange("p t (i h) -> p t i h", h=2),
-                    in_=bank[:].rearrange("p t h i -> p t i h"),
-                )
-                if last:
-                    nc.sync.dma_start(out=rows[:, tiles, :], in_=staged[:, tiles, :])
-            if not last:
-                nc.sync.dma_start(out=rows, in_=staged[:])
+                turn_back(u, half, staged, nc.scalar.copy)
+                if u >= UNITS - FINE:
+                    tiles = slice(2 * half, 2 * half + 2)
+                    nc.sync.dma_start(out=out_rows(u)[:, tiles, :], in_=staged[:, tiles, :])
+            if u < UNITS - FINE:
+                nc.sync.dma_start(out=out_rows(u), in_=staged[:])
+
+        def load_operand(u):
+            if u in new_batch:
+                for tt in range(TOKEN_TILES):
+                    load_x(new_batch[u], tt)
+            if u in new_slab:
+                for g in range(PASSES):
+                    load_w(*divmod(new_slab[u], PROJ), g)
 
         for proj in range(PROJ):
             load_bias(proj)
         load_x(0, 0)
+        load_w(0, 0, 0)
         load_x(0, 1)
-        for g in range(PASSES):
-            load_w(0, 0, g)
         load_x(0, 2)
         load_x(0, 3)
-        for g in range(PASSES):
-            load_w(0, 1, g)
-        for tt in range(TOKEN_TILES):
-            load_x(1, tt)
-        load_w(1, 0, 0)
-        for b in range(2, B):
-            for tt in range(TOKEN_TILES):
-                load_x(b, tt)
-        load_w(1, 0, 1)
-        for g in range(PASSES):
-            load_w(1, 1, g)
+        load_w(0, 0, 1)
+        for u in range(1, LOAD_AHEAD):
+            load_operand(u)
 
         index = keep.tile([P, PARTITION_BITS], I32)
         nc.gpsimd.iota(index[:], pattern=[[0, PARTITION_BITS]], base=0, channel_multiplier=1)
@@ -271,69 +309,85 @@ def tile_attention_pa_kernel(tc, x, Wq, bq, Wk, bk, out_0, out_1):
             )
         base_rate = keep.tile([P, 1], F32)
         nc.vector.tensor_reduce(out=base_rate[:], in_=factors[:], axis=mybir.AxisListType.X, op=ALU.mult)
-        rate = keep.tile([P, PAIR_TILES], F32)
-        for j in range(PAIR_TILES):
-            nc.vector.tensor_scalar(
-                out=rate[:, j : j + 1], in0=base_rate[:],
-                scalar1=THETA ** (-j * P / (E // 2)) / TWO_PI, scalar2=None, op0=ALU.mult,
-            )
+        rate = keep.tile([P, PAIR_TILES, 2], F32)
+        for phase in range(PAIR_TILES):
+            j = pair_tile(phase)
+            step_down = THETA ** (-j * P / (E // 2))
+            scales = (step_down, -step_down) if largest_angle(phase) < TWO_PI else (step_down / TWO_PI,)
+            for i, scale in enumerate(scales):
+                nc.vector.tensor_scalar(
+                    out=rate[:, j, i : i + 1], in0=base_rate[:], scalar1=scale, scalar2=None, op0=ALU.mult
+                )
 
-        make_turns(0)
         make_cos(0)
         make_sin(0)
-        make_turns(1)
+        reduce_turns(2)
 
-        transpose_x(0, 0, nc.scalar.copy)
-        transpose_x(0, 1, nc.scalar.copy)
-        for g in range(PASSES):
-            interleave_w(0, 0, g, nc.vector.tensor_copy)
+        for tt in range(TOKEN_TILES):
+            transpose_x(0, tt, nc.scalar.copy)
+        interleave_w(0, 0, 0, nc.vector.tensor_copy)
+        reduce_turns(3)
+        quantize_w(0, 0, 0, 1)
+        interleave_w(0, 0, 1, nc.vector.tensor_copy)
         for g in range(PASSES):
             quantize_x(0, g, 0, 2 * P)
-        quantize_w(0, 0)
-        transpose_x(0, 2, nc.scalar.copy)
-        transpose_x(0, 3, nc.scalar.copy)
-        make_turns(2)
+        quantize_w(0, 0, 1, 1)
+        interleave_w(0, 1, 0, nc.vector.tensor_copy)
         for g in range(PASSES):
             quantize_x(0, g, 2 * P, 2 * P)
+        interleave_w(0, 1, 1, nc.scalar.copy)
+        for tt in range(X1_BEFORE):
+            transpose_x(1, tt, nc.scalar.copy)
         multiply(0)
-        for g in range(PASSES):
-            interleave_w(0, 1, g, nc.vector.tensor_copy)
-        make_turns(3)
         quantize_w(0, 1)
-        for tt in range(TOKEN_TILES):
+        make_cos(1)
+        for tt in range(X1_BEFORE, X1_MID):
             transpose_x(1, tt, nc.scalar.copy)
 
-        for step in range(UNITS):
-            phase, offset = divmod(step, UNITS_PER_PHASE)
-            ahead = phase + 1
-            if step + 1 < UNITS:
-                multiply(step + 1)
-            if ahead < PAIR_TILES:
-                if offset == 0:
-                    make_cos(ahead)
-                if offset == 2:
-                    make_sin(ahead)
-                if offset == 1:
-                    interleave_w(ahead, 0, 0, nc.scalar.copy)
-                if offset == 5:
-                    interleave_w(ahead, 0, 1, nc.scalar.copy)
-                if offset == 6:
-                    interleave_w(ahead, 1, 0, nc.scalar.copy)
-                if offset == 7:
-                    interleave_w(ahead, 1, 1, nc.scalar.copy)
-            rotate(step)
-            b_turn, second = divmod(step + 4, 2)
-            if b_turn < B:
-                for tt in range(2 * second, 2 * second + 2):
-                    transpose_x(b_turn, tt, nc.scalar.copy)
-            if not second and b_turn - 1 < B:
+        def quantize_operand(u):
+            if u in new_batch:
                 for g in range(PASSES):
-                    quantize_x(b_turn - 1, g, 0, T)
-            if ahead < PAIR_TILES and offset >= 6:
-                quantize_w(ahead, offset - 6)
+                    quantize_x(new_batch[u], g, 0, T)
+            if u in new_slab:
+                quantize_w(*divmod(new_slab[u], PROJ))
+
+        for step in range(UNITS - 1):
+            multiply(step + 1)
+            if step == 0:
+                for tt in range(X1_MID, 4):
+                    transpose_x(1, tt, nc.scalar.copy)
+                make_sin(1)
+            for ahead in new_slab:
+                for half in range(2):
+                    if ahead > 2 and max(ahead - PREP_LEAD + half, 0) == step:
+                        interleave_w(*divmod(new_slab[ahead], PROJ), half, nc.scalar.copy)
+            for lead, make in ((TLEAD, make_cos), (TLEAD - 1, make_sin)):
+                if new_slab.get(step + lead, 1) % PROJ == 0 and step + lead > 4:
+                    make(new_slab[step + lead] // PROJ)
+            rotate(step, 0)
+            for tt in range(TOKEN_TILES):
+                ahead = step + XLEAD - tt
+                if ahead in new_batch and ahead > 2:
+                    transpose_x(new_batch[ahead], tt, nc.scalar.copy)
+            if step > 0:
+                quantize_operand(step + QUANT_LEAD)
+            rotate(step, 1)
+            if step == 0:
+                quantize_operand(step + QUANT_LEAD)
+            if not summed_on_tensor(step):
+                add_products(step)
             if step >= 2:
                 finish(step - 2)
-            if ahead + 1 < PAIR_TILES and offset >= 4:
-                load_w(ahead + 1, (offset - 4) // 2, offset % 2)
-        finish(UNITS - 2)
-        finish(UNITS - 1)
+            load_operand(step + LOAD_AHEAD)
+        last = UNITS - 1
+        staged = work.tile([P, TOKEN_TILES, 2 * P], F32, name="staged", bufs=6)
+        for h in range(2):
+            rotate(last, h, 0, 2 * P)
+        finish(last - 1)
+        finish(last - 2)
+        for h in range(2):
+            rotate(last, h, 2 * P, 2 * P)
+        for half in range(2):
+            turn_back(last, half, staged, nc.scalar.copy if half else nc.vector.tensor_copy)
+            tiles = slice(2 * half, 2 * half + 2)
+            nc.sync.dma_start(out=out_rows(last)[:, tiles, :], in_=staged[:, tiles, :])

@@ -22,33 +22,28 @@ P = 128
 PACK = 4
 K_PASS = P * PACK
 PASSES = C // K_PASS
+WORDS_PASS = K_PASS // 2
 TOKEN_TILES = T // P
-PAIR_TILES = E // (2 * P)
+HALF = T // 2
+PAIRS = E // 2
+PAIR_TILES = PAIRS // P
+SLAB = 2 * P
 PROJ = 2
-UNITS_PER_PHASE = B * PROJ
-UNITS = PAIR_TILES * UNITS_PER_PHASE
+SLABS = PAIR_TILES * PROJ
+UNITS = SLABS * B
 PARTITION_BITS = 7
 TWO_PI = 2.0 * math.pi
-LOAD_AHEAD = 13
+
+LOAD_LEAD = 13
+X_LEAD = 7
+W_LEAD = 5
+TABLE_LEAD = 4
 QUANT_LEAD = 2
-PREP_LEAD = 5
-X1_BEFORE = 1
-X1_MID = 4
-TLEAD = 4
-XLEAD = 7
-FINE = 3
-TAIL_UNITS = 2
+FINISH_LAG = 2
+TAIL = 4
 
 
-def tile_attention_pa_kernel(tc, x, Wq, bq, Wk, bk, out_0, out_1):
-    nc = tc.nc
-    weights = (Wq, Wk)
-    biases = (bq, bk)
-    outs = (out_0, out_1)
-
-    def pair_tile(phase):
-        return PAIR_TILES - 1 - phase
-
+def unit_order():
     order = [(0, 0)]
     slabs, batches = 1, 1
     while len(order) < UNITS:
@@ -58,18 +53,50 @@ def tile_attention_pa_kernel(tc, x, Wq, bq, Wk, bk, out_0, out_1):
         else:
             order += [(s, b) for b in range(batches, 2 * batches) for s in range(slabs)]
             batches *= 2
-    first_slab = {s: min(u for u in range(UNITS) if order[u][0] == s) for s in range(slabs)}
-    first_batch = {b: min(u for u in range(UNITS) if order[u][1] == b) for b in range(batches)}
-    new_slab = {u: s for s, u in first_slab.items()}
-    new_batch = {u: b for b, u in first_batch.items()}
+    return order
+
+
+def pair_tile(phase):
+    return PAIR_TILES - 1 - phase
+
+
+def first_rate(phase):
+    return THETA ** (-pair_tile(phase) * P / PAIRS)
+
+
+def largest_angle(phase):
+    return (T - 1) * first_rate(phase)
+
+
+def tile_attention_pa_kernel(tc, x, Wq, bq, Wk, bk, out_0, out_1):
+    nc = tc.nc
+    weights = (Wq, Wk)
+    biases = (bq, bk)
+    outs = (out_0, out_1)
+
+    order = unit_order()
+    first_of_slab = [min(u for u in range(UNITS) if order[u][0] == s) for s in range(SLABS)]
+    first_of_batch = [min(u for u in range(UNITS) if order[u][1] == b) for b in range(B)]
+    slab_due = [first_of_slab[s if s < SLABS // 2 else s - s % PROJ] for s in range(SLABS)]
+    quant_steps = {u - QUANT_LEAD for u in slab_due + first_of_batch}
+    interleave_at = {}
+    for s in range(PROJ, SLABS):
+        partners_behind = len([due for due in slab_due[s + 1 :] if due == slab_due[s]])
+        for g in range(PASSES):
+            step = max(slab_due[s] - W_LEAD - PASSES * partners_behind + g, 0)
+            interleave_at.setdefault(step, []).append((s, g))
 
     def unit_coords(u):
         slab, b = order[u]
         phase, proj = divmod(slab, PROJ)
-        return phase, b, proj
+        return phase, proj, b
 
-    def summed_on_tensor(u):
-        return u + QUANT_LEAD + 1 in new_slab or u + QUANT_LEAD + 1 in new_batch or u == 0 or u >= UNITS - TAIL_UNITS
+    def halves_on_tensor(u):
+        if u == 0 or u >= UNITS - TAIL // 2:
+            return 2
+        if u + 1 in quant_steps or u >= UNITS - TAIL:
+            return 1
+        return 0
 
     with ExitStack() as ctx:
         keep = ctx.enter_context(tc.tile_pool(name="keep", bufs=1))
@@ -80,27 +107,34 @@ def tile_attention_pa_kernel(tc, x, Wq, bq, Wk, bk, out_0, out_1):
         x_raw, w_raw, bias_sb = {}, {}, {}
         x_grouped, x_codes, x_scales = {}, {}, {}
         w_grouped, w_codes, w_scales = {}, {}, {}
-        turns, tables = {}, {}
+        whole, turns, tables = {}, {}, {}
         banks, products, sums = {}, {}, {}
+        freed = [[0, 1], [2, 3]]
 
         def load_x(b, tt):
-            tile = keep.tile([P, C], BF16, name="x_raw_%d_%d" % (b, tt))
-            nc.sync.dma_start(out=tile[:], in_=x[b, tt * P : (tt + 1) * P, :])
-            x_raw[b, tt] = tile
+            x_raw[b, tt] = keep.tile([P, C], BF16, name="x_raw_%d_%d" % (b, tt))
+            nc.sync.dma_start(out=x_raw[b, tt][:], in_=x[b, tt * P : (tt + 1) * P, :])
 
-        def load_w(phase, proj, g):
+        def load_w(slab, g):
+            phase, proj = divmod(slab, PROJ)
             j = pair_tile(phase)
-            tile = work.tile([P, PACK, 2 * P], BF16, name="w_raw", bufs=8)
-            rows = weights[proj][g * K_PASS : (g + 1) * K_PASS, j * 2 * P : (j + 1) * 2 * P]
-            nc.sync.dma_start(out=tile[:], in_=rows.rearrange("(p r) c -> p r c", r=PACK))
-            w_raw[phase, proj, g] = tile
+            w_raw[slab, g] = work.tile([P, PACK, SLAB], BF16, name="w_raw", bufs=8)
+            rows = weights[proj][g * K_PASS : (g + 1) * K_PASS, j * SLAB : (j + 1) * SLAB]
+            nc.sync.dma_start(out=w_raw[slab, g][:], in_=rows.rearrange("(p r) c -> p r c", r=PACK))
+
+        def load_operands(u):
+            if u in first_of_batch:
+                for tt in range(TOKEN_TILES):
+                    load_x(first_of_batch.index(u), tt)
+            if u in first_of_slab:
+                for g in range(PASSES):
+                    load_w(first_of_slab.index(u), g)
 
         def load_bias(proj):
-            tile = keep.tile([P, PAIR_TILES, 2], BF16, name="bias_%d" % proj)
-            nc.scalar.dma_start(out=tile[:], in_=biases[proj].rearrange("(j p h) -> p j h", p=P, h=2))
-            bias_sb[proj] = tile
+            bias_sb[proj] = keep.tile([P, PAIR_TILES, 2], BF16, name="bias_%d" % proj)
+            nc.scalar.dma_start(out=bias_sb[proj][:], in_=biases[proj].rearrange("(j p h) -> p j h", p=P, h=2))
 
-        def transpose_x(b, tt, copy):
+        def transpose_x(b, tt):
             if tt == 0:
                 x_grouped[b] = work.tile([P, PASSES, T * PACK], BF16, name="x_grouped", bufs=3, align_bytes=64)
                 x_codes[b] = keep.tile([P, PASSES, T], U32, name="x_codes_%d" % b, align_bytes=64)
@@ -108,131 +142,144 @@ def tile_attention_pa_kernel(tc, x, Wq, bq, Wk, bk, out_0, out_1):
             words = x_raw[b, tt][:].bitcast(F32)
             bank = psum.tile([P, PASSES, 2, P], F32, name="turn_bank")
             for g in range(PASSES):
-                for half in range(2):
-                    nc.tensor.transpose(
-                        bank[:, g, half, :], words[:, 256 * g + half : 256 * (g + 1) : 2], identity[:]
-                    )
+                for u in range(2):
+                    every_second = words[:, WORDS_PASS * g + u : WORDS_PASS * (g + 1) : 2]
+                    nc.tensor.transpose(bank[:, g, u, :], every_second, identity[:])
             target = x_grouped[b][:, :, tt * P * PACK : (tt + 1) * P * PACK].bitcast(F32)
-            copy(
+            nc.scalar.copy(
                 out=target.rearrange("p g (n u) -> p g n u", u=2),
                 in_=bank[:].rearrange("p g u n -> p g n u"),
             )
 
-        def quantize_x(b, g, first, count):
+        def quantize_x_half(b, g, half):
             nc.vector.quantize_mx(
-                out=x_codes[b][:, g, first : first + count].bitcast(E5M2),
-                scales=x_scales[b][:, g, first : first + count],
-                in_=x_grouped[b][:, g, first * PACK : (first + count) * PACK],
+                out=x_codes[b][:, g, half * HALF : (half + 1) * HALF].bitcast(E5M2),
+                scales=x_scales[b][:, g, half * HALF : (half + 1) * HALF],
+                in_=x_grouped[b][:, g, half * HALF * PACK : (half + 1) * HALF * PACK],
             )
 
-        def interleave_w(phase, proj, g, copy):
-            if g == 0:
-                w_grouped[phase, proj] = work.tile(
-                    [P, PASSES, 2 * P * PACK], BF16, name="w_grouped", align_bytes=64
-                )
+        def quantize_x(b):
+            nc.vector.quantize_mx(
+                out=x_codes[b][:].rearrange("p g n -> p (g n)").bitcast(E5M2),
+                scales=x_scales[b][:].rearrange("p g n -> p (g n)"),
+                in_=x_grouped[b][:].rearrange("p g n -> p (g n)"),
+            )
+
+        def interleave_w(slab, g, copy):
+            phase, proj = divmod(slab, PROJ)
+            if phase not in w_grouped:
+                columns = PROJ * PASSES * SLAB
+                w_grouped[phase] = work.tile([P, PROJ * PASSES, SLAB * PACK], BF16, name="w_grouped", align_bytes=64)
+                w_codes[phase] = keep.tile([P, columns], U32, name="w_codes_%d" % phase, align_bytes=64)
+                w_scales[phase] = keep.tile([P, columns], U8, name="w_scales_%d" % phase, align_bytes=64)
             copy(
-                out=w_grouped[phase, proj][:, g, :].rearrange("p (h m r) -> p h m r", h=2, r=PACK),
-                in_=w_raw[phase, proj, g][:].rearrange("p r (m h) -> p h m r", h=2),
+                out=w_grouped[phase][:, proj * PASSES + g, :].rearrange("p (h m r) -> p h m r", h=2, r=PACK),
+                in_=w_raw[slab, g][:].rearrange("p r (m h) -> p h m r", h=2),
             )
 
-        def quantize_w(phase, proj, first=0, count=PASSES):
-            if first == 0:
-                w_codes[phase, proj] = work.tile([P, PASSES * 2 * P], U32, name="w_codes", bufs=8, align_bytes=64)
-                w_scales[phase, proj] = work.tile([P, PASSES * 2 * P], U8, name="w_scales", bufs=8, align_bytes=64)
-            cols = slice(first * 2 * P, (first + count) * 2 * P)
+        def quantize_w(slab, count):
+            phase, proj = divmod(slab, PROJ)
+            first, end = proj * PASSES, (proj + count) * PASSES
             nc.vector.quantize_mx(
-                out=w_codes[phase, proj][:, cols].bitcast(E4M3),
-                scales=w_scales[phase, proj][:, cols],
-                in_=w_grouped[phase, proj][:, first : first + count, :].rearrange("p g n -> p (g n)"),
+                out=w_codes[phase][:, first * SLAB : end * SLAB].bitcast(E4M3),
+                scales=w_scales[phase][:, first * SLAB : end * SLAB],
+                in_=w_grouped[phase][:, first:end, :].rearrange("p g n -> p (g n)"),
             )
 
-        def largest_angle(phase):
-            return (T - 1) * THETA ** (-pair_tile(phase) * P / (E // 2))
+        def quantize_operands(u):
+            if u in first_of_batch:
+                quantize_x(first_of_batch.index(u))
+            if u in slab_due:
+                quantize_w(slab_due.index(u), len([due for due in slab_due if due == u]))
+
+        def count_turns(phase):
+            whole[phase] = work.tile([P, T], I32, name="whole_turns")
+            nc.vector.tensor_scalar(
+                out=whole[phase][:], in0=position[:], scalar1=rate[:, pair_tile(phase), 0:1], scalar2=None, op0=ALU.mult
+            )
 
         def reduce_turns(phase):
-            j = pair_tile(phase)
-            whole = work.tile([P, T], I32, name="whole_turns")
-            nc.vector.tensor_scalar(
-                out=whole[:], in0=position[:], scalar1=rate[:, j, 0:1], scalar2=None, op0=ALU.mult
-            )
-            tile = keep.tile([P, T], F32, name="turns_%d" % phase)
+            turns[phase] = keep.tile([P, T], F32, name="turns_%d" % phase)
             nc.vector.scalar_tensor_tensor(
-                out=tile[:], in0=position[:], scalar=rate[:, j, 0:1], in1=whole[:],
-                op0=ALU.mult, op1=ALU.subtract,
+                out=turns[phase][:],
+                in0=position[:],
+                scalar=rate[:, pair_tile(phase), 0:1],
+                in1=whole[phase][:],
+                op0=ALU.mult,
+                op1=ALU.subtract,
             )
-            turns[phase] = tile
 
         def make_cos(phase):
-            j = pair_tile(phase)
+            forward = rate[:, pair_tile(phase), 0:1]
             tables[phase] = work.tile([P, 3, T], F32, name="table", bufs=3)
-            plane = tables[phase][:, 1, :]
+            cos = tables[phase][:, 1, :]
             if largest_angle(phase) < math.pi / 2:
-                nc.scalar.activation(
-                    out=plane, in_=position[:], func=ACT.Sin, scale=rate[:, j, 0:1], bias=math.pi / 2
-                )
+                nc.scalar.activation(out=cos, in_=position[:], func=ACT.Sin, scale=forward, bias=math.pi / 2)
                 return
             magnitude = work.tile([P, T], F32, name="magnitude")
             if largest_angle(phase) < TWO_PI:
-                nc.scalar.activation(
-                    out=magnitude[:], in_=position[:], func=ACT.Abs, scale=rate[:, j, 0:1], bias=-math.pi
-                )
-                nc.scalar.activation(out=plane, in_=magnitude[:], func=ACT.Sin, bias=-math.pi / 2)
+                nc.scalar.activation(out=magnitude[:], in_=position[:], func=ACT.Abs, scale=forward, bias=-math.pi)
+                nc.scalar.activation(out=cos, in_=magnitude[:], func=ACT.Sin, bias=-math.pi / 2)
             else:
                 nc.scalar.activation(out=magnitude[:], in_=turns[phase][:], func=ACT.Abs)
-                nc.scalar.activation(out=plane, in_=magnitude[:], func=ACT.Sin, scale=-TWO_PI, bias=math.pi / 2)
+                nc.scalar.activation(out=cos, in_=magnitude[:], func=ACT.Sin, scale=-TWO_PI, bias=math.pi / 2)
 
         def make_sin(phase):
-            j = pair_tile(phase)
+            forward, backward = rate[:, pair_tile(phase), 0:1], rate[:, pair_tile(phase), 1:2]
             plus, minus = tables[phase][:, 2, :], tables[phase][:, 0, :]
             if largest_angle(phase) < math.pi / 2:
-                nc.scalar.activation(out=plus, in_=position[:], func=ACT.Sin, scale=rate[:, j, 0:1])
-                nc.scalar.activation(out=minus, in_=position[:], func=ACT.Sin, scale=rate[:, j, 1:2])
+                nc.scalar.activation(out=plus, in_=position[:], func=ACT.Sin, scale=forward)
+                nc.scalar.activation(out=minus, in_=position[:], func=ACT.Sin, scale=backward)
             elif largest_angle(phase) < TWO_PI:
-                nc.scalar.activation(out=plus, in_=position[:], func=ACT.Sin, scale=rate[:, j, 1:2], bias=math.pi)
-                nc.scalar.activation(out=minus, in_=position[:], func=ACT.Sin, scale=rate[:, j, 0:1], bias=-math.pi)
+                nc.scalar.activation(out=plus, in_=position[:], func=ACT.Sin, scale=backward, bias=math.pi)
+                nc.scalar.activation(out=minus, in_=position[:], func=ACT.Sin, scale=forward, bias=-math.pi)
             else:
                 nc.scalar.activation(out=plus, in_=turns[phase][:], func=ACT.Sin, scale=TWO_PI)
                 nc.scalar.activation(out=minus, in_=turns[phase][:], func=ACT.Sin, scale=-TWO_PI)
 
         def multiply(u):
-            phase, b, proj = unit_coords(u)
-            for h in range(2):
-                bank = psum.tile([P, T], F32, name="mx_bank")
+            phase, proj, b = unit_coords(u)
+            written = (0, 1) if u == 0 else (1, 0)
+            places = freed[u % 2]
+            freed[u % 2] = [places[written.index(h)] for h in range(2)]
+            for h, place in zip(written, places):
+                banks[u, h] = psum.tile([P, T], F32, name="mx_bank_%d" % place, bufs=1)
                 for g in range(PASSES):
-                    cols = slice((2 * g + h) * P, (2 * g + h + 1) * P)
+                    block = 2 * (proj * PASSES + g) + h
+                    cols = slice(block * P, (block + 1) * P)
                     nc.tensor.matmul_mx(
-                        out=bank[:],
-                        lhsT=w_codes[phase, proj][:, cols].bitcast(E4M3),
-                        lhsT_scale=w_scales[phase, proj][:, cols],
+                        out=banks[u, h][:],
+                        lhsT=w_codes[phase][:, cols].bitcast(E4M3),
+                        lhsT_scale=w_scales[phase][:, cols],
                         rhs=x_codes[b][:, g, :].bitcast(E5M2),
                         rhs_scale=x_scales[b][:, g, :],
                         start=(g == 0),
                         stop=(g == PASSES - 1),
                     )
-                banks[u, h] = bank
 
-        def rotate(u, h, first=0, count=T):
-            phase, b, proj = unit_coords(u)
-            j = pair_tile(phase)
+        def rotate(u, h, first, count):
+            phase, proj, b = unit_coords(u)
             if first == 0:
-                products[u, h] = work.tile([P, 2, T], F32, name="product", bufs=8)
+                products[u, h] = work.tile([P, 2, T], F32, name="product", bufs=10)
             cols = slice(first, first + count)
             nc.vector.scalar_tensor_tensor(
                 out=products[u, h][:, :, cols],
                 in0=banks[u, h][:, cols].unsqueeze(1).to_broadcast([P, 2, count]),
-                scalar=bias_sb[proj][:, j, h : h + 1],
+                scalar=bias_sb[proj][:, pair_tile(phase), h : h + 1],
                 in1=tables[phase][:, 1 - h : 3 - h, cols],
                 op0=ALU.add,
                 op1=ALU.mult,
             )
 
         def add_products(u):
-            total = work.tile([P, 2, T], F32, name="total", bufs=3)
-            nc.gpsimd.tensor_tensor(out=total[:], in0=products[u, 0][:], in1=products[u, 1][:], op=ALU.add)
-            sums[u] = total
+            sums[u] = work.tile([P, 2, T], F32, name="total", bufs=3)
+            cols = slice(halves_on_tensor(u) * HALF, T)
+            nc.gpsimd.tensor_tensor(
+                out=sums[u][:, :, cols], in0=products[u, 0][:, :, cols], in1=products[u, 1][:, :, cols], op=ALU.add
+            )
 
         def turn_back(u, half, staged, copy):
-            terms = [products[u, 0], products[u, 1]] if summed_on_tensor(u) else [sums[u]]
+            terms = [products[u, 0], products[u, 1]] if half < halves_on_tensor(u) else [sums[u]]
             bank = psum.tile([P, 2, 2, P], F32, name="turn_bank")
             for k in range(2):
                 tt = 2 * half + k
@@ -251,39 +298,35 @@ def tile_attention_pa_kernel(tc, x, Wq, bq, Wk, bk, out_0, out_1):
                 in_=bank[:].rearrange("p t h i -> p t i h"),
             )
 
-        def out_rows(u):
-            phase, b, proj = unit_coords(u)
+        def store(u, staged, tiles):
+            phase, proj, b = unit_coords(u)
             j = pair_tile(phase)
-            return outs[proj][b, :, j * 2 * P : (j + 1) * 2 * P].rearrange("(t p) c -> p t c", p=P)
+            rows = outs[proj][b, :, j * SLAB : (j + 1) * SLAB].rearrange("(t p) c -> p t c", p=P)
+            nc.sync.dma_start(out=rows[:, tiles, :], in_=staged[:, tiles, :])
+
+        def new_staging():
+            staged = work.tile([P, TOKEN_TILES, SLAB], F32, name="staged", bufs=6)
+            return staged
 
         def finish(u):
-            staged = work.tile([P, TOKEN_TILES, 2 * P], F32, name="staged", bufs=6)
+            by_halves = u >= UNITS - TAIL - 1
+            staged = new_staging()
             for half in range(2):
                 turn_back(u, half, staged, nc.scalar.copy)
-                if u >= UNITS - FINE:
-                    tiles = slice(2 * half, 2 * half + 2)
-                    nc.sync.dma_start(out=out_rows(u)[:, tiles, :], in_=staged[:, tiles, :])
-            if u < UNITS - FINE:
-                nc.sync.dma_start(out=out_rows(u), in_=staged[:])
-
-        def load_operand(u):
-            if u in new_batch:
-                for tt in range(TOKEN_TILES):
-                    load_x(new_batch[u], tt)
-            if u in new_slab:
-                for g in range(PASSES):
-                    load_w(*divmod(new_slab[u], PROJ), g)
+                if by_halves:
+                    store(u, staged, slice(2 * half, 2 * half + 2))
+            if not by_halves:
+                store(u, staged, slice(0, TOKEN_TILES))
 
         for proj in range(PROJ):
             load_bias(proj)
         load_x(0, 0)
-        load_w(0, 0, 0)
-        load_x(0, 1)
-        load_x(0, 2)
-        load_x(0, 3)
-        load_w(0, 0, 1)
-        for u in range(1, LOAD_AHEAD):
-            load_operand(u)
+        load_w(0, 0)
+        for tt in range(1, TOKEN_TILES):
+            load_x(0, tt)
+        load_w(0, 1)
+        for u in range(1, LOAD_LEAD):
+            load_operands(u)
 
         index = keep.tile([P, PARTITION_BITS], I32)
         nc.gpsimd.iota(index[:], pattern=[[0, PARTITION_BITS]], base=0, channel_multiplier=1)
@@ -302,92 +345,82 @@ def tile_attention_pa_kernel(tc, x, Wq, bq, Wk, bk, out_0, out_1):
         nc.vector.tensor_scalar(out=bits[:], in0=shifted[:], scalar1=1, scalar2=None, op0=ALU.bitwise_and)
         factors = keep.tile([P, PARTITION_BITS], F32)
         for bit in range(PARTITION_BITS):
-            ratio = THETA ** (-(2**bit) / (E // 2))
             nc.vector.tensor_scalar(
-                out=factors[:, bit : bit + 1], in0=bits[:, bit : bit + 1],
-                scalar1=ratio - 1.0, scalar2=1.0, op0=ALU.mult, op1=ALU.add,
+                out=factors[:, bit : bit + 1],
+                in0=bits[:, bit : bit + 1],
+                scalar1=THETA ** (-(2**bit) / PAIRS) - 1.0,
+                scalar2=1.0,
+                op0=ALU.mult,
+                op1=ALU.add,
             )
         base_rate = keep.tile([P, 1], F32)
         nc.vector.tensor_reduce(out=base_rate[:], in_=factors[:], axis=mybir.AxisListType.X, op=ALU.mult)
         rate = keep.tile([P, PAIR_TILES, 2], F32)
+        reduced = [phase for phase in range(PAIR_TILES) if largest_angle(phase) >= TWO_PI]
         for phase in range(PAIR_TILES):
-            j = pair_tile(phase)
-            step_down = THETA ** (-j * P / (E // 2))
-            scales = (step_down, -step_down) if largest_angle(phase) < TWO_PI else (step_down / TWO_PI,)
-            for i, scale in enumerate(scales):
+            radians = first_rate(phase)
+            for i, scale in enumerate((radians / TWO_PI,) if phase in reduced else (radians, -radians)):
                 nc.vector.tensor_scalar(
-                    out=rate[:, j, i : i + 1], in0=base_rate[:], scalar1=scale, scalar2=None, op0=ALU.mult
+                    out=rate[:, pair_tile(phase), i : i + 1], in0=base_rate[:], scalar1=scale, scalar2=None, op0=ALU.mult
                 )
 
         make_cos(0)
         make_sin(0)
-        reduce_turns(2)
+        for phase in reduced:
+            count_turns(phase)
+        for phase in reduced:
+            reduce_turns(phase)
 
         for tt in range(TOKEN_TILES):
-            transpose_x(0, tt, nc.scalar.copy)
-        interleave_w(0, 0, 0, nc.vector.tensor_copy)
-        reduce_turns(3)
-        quantize_w(0, 0, 0, 1)
-        interleave_w(0, 0, 1, nc.vector.tensor_copy)
+            transpose_x(0, tt)
         for g in range(PASSES):
-            quantize_x(0, g, 0, 2 * P)
-        quantize_w(0, 0, 1, 1)
-        interleave_w(0, 1, 0, nc.vector.tensor_copy)
-        for g in range(PASSES):
-            quantize_x(0, g, 2 * P, 2 * P)
-        interleave_w(0, 1, 1, nc.scalar.copy)
-        for tt in range(X1_BEFORE):
-            transpose_x(1, tt, nc.scalar.copy)
-        multiply(0)
+            interleave_w(0, g, nc.vector.tensor_copy)
+            quantize_x_half(0, g, 0)
         quantize_w(0, 1)
+        for g in range(PASSES):
+            quantize_x_half(0, g, 1)
+        interleave_w(1, 0, nc.vector.tensor_copy)
+        interleave_w(1, 1, nc.scalar.copy)
+        transpose_x(1, 0)
+        multiply(0)
+        quantize_w(1, 1)
         make_cos(1)
-        for tt in range(X1_BEFORE, X1_MID):
-            transpose_x(1, tt, nc.scalar.copy)
+        for tt in range(1, TOKEN_TILES):
+            transpose_x(1, tt)
 
-        def quantize_operand(u):
-            if u in new_batch:
-                for g in range(PASSES):
-                    quantize_x(new_batch[u], g, 0, T)
-            if u in new_slab:
-                quantize_w(*divmod(new_slab[u], PROJ))
-
+        finished = 0
         for step in range(UNITS - 1):
             multiply(step + 1)
             if step == 0:
-                for tt in range(X1_MID, 4):
-                    transpose_x(1, tt, nc.scalar.copy)
                 make_sin(1)
-            for ahead in new_slab:
-                for half in range(2):
-                    if ahead > 2 and max(ahead - PREP_LEAD + half, 0) == step:
-                        interleave_w(*divmod(new_slab[ahead], PROJ), half, nc.scalar.copy)
-            for lead, make in ((TLEAD, make_cos), (TLEAD - 1, make_sin)):
-                if new_slab.get(step + lead, 1) % PROJ == 0 and step + lead > 4:
-                    make(new_slab[step + lead] // PROJ)
-            rotate(step, 0)
-            for tt in range(TOKEN_TILES):
-                ahead = step + XLEAD - tt
-                if ahead in new_batch and ahead > 2:
-                    transpose_x(new_batch[ahead], tt, nc.scalar.copy)
-            if step > 0:
-                quantize_operand(step + QUANT_LEAD)
-            rotate(step, 1)
-            if step == 0:
-                quantize_operand(step + QUANT_LEAD)
-            if not summed_on_tensor(step):
+            for slab, g in interleave_at.get(step, []):
+                interleave_w(slab, g, nc.scalar.copy)
+            for phase in reduced:
+                if step == first_of_slab[PROJ * phase] - TABLE_LEAD:
+                    make_cos(phase)
+                if step == first_of_slab[PROJ * phase] - TABLE_LEAD + 1:
+                    make_sin(phase)
+            rotate(step, 0, 0, T)
+            for b in range(2, B):
+                tt = step - (first_of_batch[b] - X_LEAD)
+                if 0 <= tt < TOKEN_TILES:
+                    transpose_x(b, tt)
+            rotate(step, 1, 0, T)
+            quantize_operands(step + QUANT_LEAD)
+            if halves_on_tensor(step) < 2:
                 add_products(step)
-            if step >= 2:
-                finish(step - 2)
-            load_operand(step + LOAD_AHEAD)
+            while finished <= step - (FINISH_LAG if finished < UNITS - TAIL else FINISH_LAG - 1):
+                finish(finished)
+                finished += 1
+            load_operands(step + LOAD_LEAD)
+
         last = UNITS - 1
-        staged = work.tile([P, TOKEN_TILES, 2 * P], F32, name="staged", bufs=6)
+        staged = new_staging()
         for h in range(2):
-            rotate(last, h, 0, 2 * P)
+            rotate(last, h, 0, HALF)
         finish(last - 1)
-        finish(last - 2)
         for h in range(2):
-            rotate(last, h, 2 * P, 2 * P)
-        for half in range(2):
-            turn_back(last, half, staged, nc.scalar.copy if half else nc.vector.tensor_copy)
-            tiles = slice(2 * half, 2 * half + 2)
-            nc.sync.dma_start(out=out_rows(last)[:, tiles, :], in_=staged[:, tiles, :])
+            rotate(last, h, HALF, HALF)
+        for half, copy in enumerate((nc.vector.tensor_copy, nc.scalar.copy)):
+            turn_back(last, half, staged, copy)
+            store(last, staged, slice(2 * half, 2 * half + 2))

@@ -36,11 +36,13 @@ TWO_PI = 2.0 * math.pi
 
 LOAD_LEAD = 13
 X_LEAD = 7
-W_LEAD = 5
 TABLE_LEAD = 4
-QUANT_LEAD = 2
+QUANT_LEAD = 3
+EARLY = 8
+W_LEAD = 3
 FINISH_LAG = 2
-TAIL = 4
+TAIL = 2
+HALF_STORES = 5
 
 
 def unit_order():
@@ -77,26 +79,26 @@ def tile_attention_pa_kernel(tc, x, Wq, bq, Wk, bk, out_0, out_1):
     order = unit_order()
     first_of_slab = [min(u for u in range(UNITS) if order[u][0] == s) for s in range(SLABS)]
     first_of_batch = [min(u for u in range(UNITS) if order[u][1] == b) for b in range(B)]
-    slab_due = [first_of_slab[s if s < SLABS // 2 else s - s % PROJ] for s in range(SLABS)]
-    quant_steps = {u - QUANT_LEAD for u in slab_due + first_of_batch}
-    interleave_at = {}
-    for s in range(PROJ, SLABS):
-        partners_behind = len([due for due in slab_due[s + 1 :] if due == slab_due[s]])
-        for g in range(PASSES):
-            step = max(slab_due[s] - W_LEAD - PASSES * partners_behind + g, 0)
-            interleave_at.setdefault(step, []).append((s, g))
+
+    def quant_step(first_unit):
+        return first_unit - (QUANT_LEAD - 1 if first_unit < EARLY else QUANT_LEAD)
+
+    slab_at = {quant_step(first_of_slab[s]): s for s in range(PROJ, SLABS)}
+    batch_at = {quant_step(first_of_batch[b]): b for b in range(1, B)}
+    quant_steps = set(slab_at) | set(batch_at)
 
     def unit_coords(u):
         slab, b = order[u]
         phase, proj = divmod(slab, PROJ)
         return phase, proj, b
 
+    def odd_on_gpsimd(u):
+        return u - 1 in quant_steps and u > EARLY
+
     def halves_on_tensor(u):
-        if u == 0 or u >= UNITS - TAIL // 2:
+        if u == 0 or odd_on_gpsimd(u) or u >= UNITS - TAIL:
             return 2
-        if u + 1 in quant_steps or u >= UNITS - TAIL:
-            return 1
-        return 0
+        return 1 if u + 1 in quant_steps else 0
 
     with ExitStack() as ctx:
         keep = ctx.enter_context(tc.tile_pool(name="keep", bufs=1))
@@ -108,8 +110,7 @@ def tile_attention_pa_kernel(tc, x, Wq, bq, Wk, bk, out_0, out_1):
         x_grouped, x_codes, x_scales = {}, {}, {}
         w_grouped, w_codes, w_scales = {}, {}, {}
         whole, turns, tables = {}, {}, {}
-        banks, products, sums = {}, {}, {}
-        freed = [[0, 1], [2, 3]]
+        banks, biased, products, sums = {}, {}, {}, {}
 
         def load_x(b, tt):
             x_raw[b, tt] = keep.tile([P, C], BF16, name="x_raw_%d_%d" % (b, tt))
@@ -177,20 +178,14 @@ def tile_attention_pa_kernel(tc, x, Wq, bq, Wk, bk, out_0, out_1):
                 in_=w_raw[slab, g][:].rearrange("p r (m h) -> p h m r", h=2),
             )
 
-        def quantize_w(slab, count):
+        def quantize_w(slab):
             phase, proj = divmod(slab, PROJ)
-            first, end = proj * PASSES, (proj + count) * PASSES
+            first, end = proj * PASSES, (proj + 1) * PASSES
             nc.vector.quantize_mx(
                 out=w_codes[phase][:, first * SLAB : end * SLAB].bitcast(E4M3),
                 scales=w_scales[phase][:, first * SLAB : end * SLAB],
                 in_=w_grouped[phase][:, first:end, :].rearrange("p g n -> p (g n)"),
             )
-
-        def quantize_operands(u):
-            if u in first_of_batch:
-                quantize_x(first_of_batch.index(u))
-            if u in slab_due:
-                quantize_w(slab_due.index(u), len([due for due in slab_due if due == u]))
 
         def count_turns(phase):
             whole[phase] = work.tile([P, T], I32, name="whole_turns")
@@ -239,11 +234,8 @@ def tile_attention_pa_kernel(tc, x, Wq, bq, Wk, bk, out_0, out_1):
 
         def multiply(u):
             phase, proj, b = unit_coords(u)
-            written = (0, 1) if u == 0 else (1, 0)
-            places = freed[u % 2]
-            freed[u % 2] = [places[written.index(h)] for h in range(2)]
-            for h, place in zip(written, places):
-                banks[u, h] = psum.tile([P, T], F32, name="mx_bank_%d" % place, bufs=1)
+            for h in range(2):
+                banks[u, h] = psum.tile([P, T], F32, name="mx_bank")
                 for g in range(PASSES):
                     block = 2 * (proj * PASSES + g) + h
                     cols = slice(block * P, (block + 1) * P)
@@ -257,10 +249,27 @@ def tile_attention_pa_kernel(tc, x, Wq, bq, Wk, bk, out_0, out_1):
                         stop=(g == PASSES - 1),
                     )
 
+        def take_odd(u):
+            phase, proj, b = unit_coords(u)
+            biased[u] = work.tile([P, T], F32, name="biased", bufs=1)
+            nc.scalar.activation(
+                out=biased[u][:], in_=banks[u, 1][:], func=ACT.Identity, bias=bias_sb[proj][:, pair_tile(phase), 1:2]
+            )
+
+        def rotate_odd_on_gpsimd(u):
+            phase, proj, b = unit_coords(u)
+            products[u, 1] = work.tile([P, 2, T], F32, name="product", bufs=8)
+            nc.gpsimd.tensor_tensor(
+                out=products[u, 1][:],
+                in0=biased[u][:].unsqueeze(1).to_broadcast([P, 2, T]),
+                in1=tables[phase][:, 0:2, :],
+                op=ALU.mult,
+            )
+
         def rotate(u, h, first, count):
             phase, proj, b = unit_coords(u)
             if first == 0:
-                products[u, h] = work.tile([P, 2, T], F32, name="product", bufs=10)
+                products[u, h] = work.tile([P, 2, T], F32, name="product", bufs=8)
             cols = slice(first, first + count)
             nc.vector.scalar_tensor_tensor(
                 out=products[u, h][:, :, cols],
@@ -309,7 +318,7 @@ def tile_attention_pa_kernel(tc, x, Wq, bq, Wk, bk, out_0, out_1):
             return staged
 
         def finish(u):
-            by_halves = u >= UNITS - TAIL - 1
+            by_halves = u >= UNITS - HALF_STORES
             staged = new_staging()
             for half in range(2):
                 turn_back(u, half, staged, nc.scalar.copy)
@@ -376,25 +385,28 @@ def tile_attention_pa_kernel(tc, x, Wq, bq, Wk, bk, out_0, out_1):
         for g in range(PASSES):
             interleave_w(0, g, nc.vector.tensor_copy)
             quantize_x_half(0, g, 0)
-        quantize_w(0, 1)
+        quantize_w(0)
         for g in range(PASSES):
             quantize_x_half(0, g, 1)
         interleave_w(1, 0, nc.vector.tensor_copy)
         interleave_w(1, 1, nc.scalar.copy)
         transpose_x(1, 0)
         multiply(0)
-        quantize_w(1, 1)
+        quantize_w(1)
         make_cos(1)
         for tt in range(1, TOKEN_TILES):
             transpose_x(1, tt)
 
-        finished = 0
         for step in range(UNITS - 1):
             multiply(step + 1)
+            if odd_on_gpsimd(step + 1):
+                take_odd(step + 1)
             if step == 0:
                 make_sin(1)
-            for slab, g in interleave_at.get(step, []):
-                interleave_w(slab, g, nc.scalar.copy)
+            for at in slab_at:
+                for g in range(PASSES):
+                    if step == max(at - W_LEAD + g, 0):
+                        interleave_w(slab_at[at], g, nc.scalar.copy)
             for phase in reduced:
                 if step == first_of_slab[PROJ * phase] - TABLE_LEAD:
                     make_cos(phase)
@@ -405,13 +417,18 @@ def tile_attention_pa_kernel(tc, x, Wq, bq, Wk, bk, out_0, out_1):
                 tt = step - (first_of_batch[b] - X_LEAD)
                 if 0 <= tt < TOKEN_TILES:
                     transpose_x(b, tt)
-            rotate(step, 1, 0, T)
-            quantize_operands(step + QUANT_LEAD)
+            if odd_on_gpsimd(step):
+                rotate_odd_on_gpsimd(step)
+            else:
+                rotate(step, 1, 0, T)
+            if step in batch_at:
+                quantize_x(batch_at[step])
+            if step in slab_at:
+                quantize_w(slab_at[step])
             if halves_on_tensor(step) < 2:
                 add_products(step)
-            while finished <= step - (FINISH_LAG if finished < UNITS - TAIL else FINISH_LAG - 1):
-                finish(finished)
-                finished += 1
+            if step >= FINISH_LAG:
+                finish(step - FINISH_LAG)
             load_operands(step + LOAD_LEAD)
 
         last = UNITS - 1
@@ -419,6 +436,7 @@ def tile_attention_pa_kernel(tc, x, Wq, bq, Wk, bk, out_0, out_1):
         for h in range(2):
             rotate(last, h, 0, HALF)
         finish(last - 1)
+        finish(last - 2)
         for h in range(2):
             rotate(last, h, HALF, HALF)
         for half, copy in enumerate((nc.vector.tensor_copy, nc.scalar.copy)):

@@ -41,7 +41,7 @@ QUANT_LEAD = 3
 EARLY = 8
 W_LEAD = 3
 FINISH_LAG = 2
-TAIL = 2
+TAIL = 4
 HALF_STORES = 5
 
 
@@ -92,13 +92,10 @@ def tile_attention_pa_kernel(tc, x, Wq, bq, Wk, bk, out_0, out_1):
         phase, proj = divmod(slab, PROJ)
         return phase, proj, b
 
-    def odd_on_gpsimd(u):
-        return u - 1 in quant_steps and u > EARLY
-
     def halves_on_tensor(u):
-        if u == 0 or odd_on_gpsimd(u) or u >= UNITS - TAIL:
+        if u == 0 or u >= UNITS - TAIL // 2:
             return 2
-        return 1 if u + 1 in quant_steps else 0
+        return 1 if (u % 2 == 0 and u > 2) or u + 1 in quant_steps or u >= UNITS - TAIL else 0
 
     with ExitStack() as ctx:
         keep = ctx.enter_context(tc.tile_pool(name="keep", bufs=1))
@@ -106,11 +103,11 @@ def tile_attention_pa_kernel(tc, x, Wq, bq, Wk, bk, out_0, out_1):
         psum = ctx.enter_context(tc.psum_pool(name="psum", bufs=4))
         ctx.enter_context(tc.manual_schedule())
 
-        x_raw, w_raw, bias_sb = {}, {}, {}
+        x_raw, w_raw = {}, {}
         x_grouped, x_codes, x_scales = {}, {}, {}
         w_grouped, w_codes, w_scales = {}, {}, {}
         whole, turns, tables = {}, {}, {}
-        banks, biased, products, sums = {}, {}, {}, {}
+        banks, products, sums = {}, {}, {}
 
         def load_x(b, tt):
             x_raw[b, tt] = keep.tile([P, C], BF16, name="x_raw_%d_%d" % (b, tt))
@@ -130,10 +127,6 @@ def tile_attention_pa_kernel(tc, x, Wq, bq, Wk, bk, out_0, out_1):
             if u in first_of_slab:
                 for g in range(PASSES):
                     load_w(first_of_slab.index(u), g)
-
-        def load_bias(proj):
-            bias_sb[proj] = keep.tile([P, PAIR_TILES, 2], BF16, name="bias_%d" % proj)
-            nc.scalar.dma_start(out=bias_sb[proj][:], in_=biases[proj].rearrange("(j p h) -> p j h", p=P, h=2))
 
         def transpose_x(b, tt):
             if tt == 0:
@@ -174,8 +167,8 @@ def tile_attention_pa_kernel(tc, x, Wq, bq, Wk, bk, out_0, out_1):
                 w_codes[phase] = keep.tile([P, columns], U32, name="w_codes_%d" % phase, align_bytes=64)
                 w_scales[phase] = keep.tile([P, columns], U8, name="w_scales_%d" % phase, align_bytes=64)
             copy(
-                out=w_grouped[phase][:, proj * PASSES + g, :].rearrange("p (h m r) -> p h m r", h=2, r=PACK),
-                in_=w_raw[slab, g][:].rearrange("p r (m h) -> p h m r", h=2),
+                out=w_grouped[phase][:, proj * PASSES + g, :].rearrange("p (h c i r) -> p h c r i", h=2, i=4, r=PACK),
+                in_=w_raw[slab, g][:].rearrange("p r (c i h) -> p h c r i", h=2, i=4),
             )
 
         def quantize_w(slab):
@@ -249,23 +242,6 @@ def tile_attention_pa_kernel(tc, x, Wq, bq, Wk, bk, out_0, out_1):
                         stop=(g == PASSES - 1),
                     )
 
-        def take_odd(u):
-            phase, proj, b = unit_coords(u)
-            biased[u] = work.tile([P, T], F32, name="biased", bufs=1)
-            nc.scalar.activation(
-                out=biased[u][:], in_=banks[u, 1][:], func=ACT.Identity, bias=bias_sb[proj][:, pair_tile(phase), 1:2]
-            )
-
-        def rotate_odd_on_gpsimd(u):
-            phase, proj, b = unit_coords(u)
-            products[u, 1] = work.tile([P, 2, T], F32, name="product", bufs=8)
-            nc.gpsimd.tensor_tensor(
-                out=products[u, 1][:],
-                in0=biased[u][:].unsqueeze(1).to_broadcast([P, 2, T]),
-                in1=tables[phase][:, 0:2, :],
-                op=ALU.mult,
-            )
-
         def rotate(u, h, first, count):
             phase, proj, b = unit_coords(u)
             if first == 0:
@@ -274,7 +250,7 @@ def tile_attention_pa_kernel(tc, x, Wq, bq, Wk, bk, out_0, out_1):
             nc.vector.scalar_tensor_tensor(
                 out=products[u, h][:, :, cols],
                 in0=banks[u, h][:, cols].unsqueeze(1).to_broadcast([P, 2, count]),
-                scalar=bias_sb[proj][:, pair_tile(phase), h : h + 1],
+                scalar=bias_sb[:, proj, pair_tile(phase), h : h + 1],
                 in1=tables[phase][:, 1 - h : 3 - h, cols],
                 op0=ALU.add,
                 op1=ALU.mult,
@@ -327,8 +303,13 @@ def tile_attention_pa_kernel(tc, x, Wq, bq, Wk, bk, out_0, out_1):
             if not by_halves:
                 store(u, staged, slice(0, TOKEN_TILES))
 
+        bias_rows = keep.tile([P, SLAB], BF16)
+        nc.vector.memset(bias_rows[:], 0.0)
         for proj in range(PROJ):
-            load_bias(proj)
+            nc.scalar.dma_start(
+                out=bias_rows[proj * PAIR_TILES : (proj + 1) * PAIR_TILES, :],
+                in_=biases[proj].rearrange("(j c) -> j c", j=PAIR_TILES),
+            )
         load_x(0, 0)
         load_w(0, 0)
         for tt in range(1, TOKEN_TILES):
@@ -382,6 +363,10 @@ def tile_attention_pa_kernel(tc, x, Wq, bq, Wk, bk, out_0, out_1):
 
         for tt in range(TOKEN_TILES):
             transpose_x(0, tt)
+        bias_bank = psum.tile([P, PASSES, 2, P], F32, name="turn_bank")
+        nc.tensor.transpose(bias_bank[:, 0, 0, :], bias_rows[:].bitcast(F32), identity[:])
+        bias_sb = keep.tile([P, PROJ, PAIR_TILES, 2], BF16)
+        nc.scalar.copy(out=bias_sb[:].rearrange("p a j h -> p (a j h)").bitcast(F32), in_=bias_bank[:, 0, 0, 0:SLABS])
         for g in range(PASSES):
             interleave_w(0, g, nc.vector.tensor_copy)
             quantize_x_half(0, g, 0)
@@ -397,10 +382,9 @@ def tile_attention_pa_kernel(tc, x, Wq, bq, Wk, bk, out_0, out_1):
         for tt in range(1, TOKEN_TILES):
             transpose_x(1, tt)
 
+        finished = 0
         for step in range(UNITS - 1):
             multiply(step + 1)
-            if odd_on_gpsimd(step + 1):
-                take_odd(step + 1)
             if step == 0:
                 make_sin(1)
             for at in slab_at:
@@ -417,18 +401,16 @@ def tile_attention_pa_kernel(tc, x, Wq, bq, Wk, bk, out_0, out_1):
                 tt = step - (first_of_batch[b] - X_LEAD)
                 if 0 <= tt < TOKEN_TILES:
                     transpose_x(b, tt)
-            if odd_on_gpsimd(step):
-                rotate_odd_on_gpsimd(step)
-            else:
-                rotate(step, 1, 0, T)
+            rotate(step, 1, 0, T)
             if step in batch_at:
                 quantize_x(batch_at[step])
             if step in slab_at:
                 quantize_w(slab_at[step])
             if halves_on_tensor(step) < 2:
                 add_products(step)
-            if step >= FINISH_LAG:
-                finish(step - FINISH_LAG)
+            while finished <= step - (FINISH_LAG if finished < UNITS - TAIL else FINISH_LAG - 1):
+                finish(finished)
+                finished += 1
             load_operands(step + LOAD_LEAD)
 
         last = UNITS - 1
@@ -436,7 +418,6 @@ def tile_attention_pa_kernel(tc, x, Wq, bq, Wk, bk, out_0, out_1):
         for h in range(2):
             rotate(last, h, 0, HALF)
         finish(last - 1)
-        finish(last - 2)
         for h in range(2):
             rotate(last, h, HALF, HALF)
         for half, copy in enumerate((nc.vector.tensor_copy, nc.scalar.copy)):

import math
from contextlib import ExitStack

import concourse.mybir as mybir
from concourse.masks import make_identity

B, T, C, E = 4, 512, 1024, 1024
THETA = 10000.0
FLOPS = 2 * 2 * B * T * C * E

F32 = mybir.dt.float32
BF16 = mybir.dt.bfloat16
I32 = mybir.dt.int32
U32 = mybir.dt.uint32
U8 = mybir.dt.uint8
E4M3 = mybir.dt.float8_e4m3fn_x4
E5M2 = mybir.dt.float8_e5m2_x4
ALU = mybir.AluOpType
ACT = mybir.ActivationFunctionType

P = 128
PACK = 4
K_PASS = P * PACK
PASSES = C // K_PASS
WORDS_PASS = K_PASS // 2
TOKEN_TILES = T // P
HALF = T // 2
PAIRS = E // 2
PAIR_TILES = PAIRS // P
SLAB = 2 * P
PROJ = 2
SLABS = PAIR_TILES * PROJ
UNITS = SLABS * B
PARTITION_BITS = 7
TWO_PI = 2.0 * math.pi

LOAD_LEAD = 13
X_LEAD = 7
TABLE_LEAD = 4
QUANT_LEAD = 3
EARLY = 8
W_LEAD = 3
FINISH_LAG = 2
TAIL = 4
HALF_STORES = 5


def unit_order():
    order = [(0, 0)]
    slabs, batches = 1, 1
    while len(order) < UNITS:
        if slabs == batches:
            order += [(s, b) for s in range(slabs, 2 * slabs) for b in range(batches)]
            slabs *= 2
        else:
            order += [(s, b) for b in range(batches, 2 * batches) for s in range(slabs)]
            batches *= 2
    return order


def pair_tile(phase):
    return PAIR_TILES - 1 - phase


def first_rate(phase):
    return THETA ** (-pair_tile(phase) * P / PAIRS)


def largest_angle(phase):
    return (T - 1) * first_rate(phase)


def tile_attention_pa_kernel(tc, x, Wq, bq, Wk, bk, out_0, out_1):
    nc = tc.nc
    weights = (Wq, Wk)
    biases = (bq, bk)
    outs = (out_0, out_1)

    order = unit_order()
    first_of_slab = [min(u for u in range(UNITS) if order[u][0] == s) for s in range(SLABS)]
    first_of_batch = [min(u for u in range(UNITS) if order[u][1] == b) for b in range(B)]

    def quant_step(first_unit):
        return first_unit - (QUANT_LEAD - 1 if first_unit < EARLY else QUANT_LEAD)

    slab_at = {quant_step(first_of_slab[s]): s for s in range(PROJ, SLABS)}
    batch_at = {quant_step(first_of_batch[b]): b for b in range(1, B)}
    quant_steps = set(slab_at) | set(batch_at)

    def unit_coords(u):
        slab, b = order[u]
        phase, proj = divmod(slab, PROJ)
        return phase, proj, b

    def halves_on_tensor(u):
        if u == 0 or u >= UNITS - TAIL // 2:
            return 2
        return 1 if (u % 2 == 0 and u > 2) or u + 1 in quant_steps or u >= UNITS - TAIL else 0

    with ExitStack() as ctx:
        keep = ctx.enter_context(tc.tile_pool(name="keep", bufs=1))
        work = ctx.enter_context(tc.tile_pool(name="work", bufs=2))
        psum = ctx.enter_context(tc.psum_pool(name="psum", bufs=4))
        ctx.enter_context(tc.manual_schedule())

        x_raw, w_raw = {}, {}
        x_grouped, x_codes, x_scales = {}, {}, {}
        w_grouped, w_codes, w_scales = {}, {}, {}
        whole, turns, tables = {}, {}, {}
        banks, products, sums = {}, {}, {}

        def load_x(b, tt):
            x_raw[b, tt] = keep.tile([P, C], BF16, name="x_raw_%d_%d" % (b, tt))
            nc.sync.dma_start(out=x_raw[b, tt][:], in_=x[b, tt * P : (tt + 1) * P, :])

        def load_w(slab, g):
            phase, proj = divmod(slab, PROJ)
            j = pair_tile(phase)
            w_raw[slab, g] = work.tile([P, PACK, SLAB], BF16, name="w_raw", bufs=8)
            rows = weights[proj][g * K_PASS : (g + 1) * K_PASS, j * SLAB : (j + 1) * SLAB]
            nc.sync.dma_start(out=w_raw[slab, g][:], in_=rows.rearrange("(p r) c -> p r c", r=PACK))

        def load_operands(u):
            if u in first_of_batch:
                for tt in range(TOKEN_TILES):
                    load_x(first_of_batch.index(u), tt)
            if u in first_of_slab:
                for g in range(PASSES):
                    load_w(first_of_slab.index(u), g)

        def transpose_x(b, tt):
            if tt == 0:
                x_grouped[b] = work.tile([P, PASSES, T * PACK], BF16, name="x_grouped", bufs=3, align_bytes=64)
                x_codes[b] = keep.tile([P, PASSES, T], U32, name="x_codes_%d" % b, align_bytes=64)
                x_scales[b] = keep.tile([P, PASSES, T], U8, name="x_scales_%d" % b, align_bytes=64)
            words = x_raw[b, tt][:].bitcast(F32)
            bank = psum.tile([P, PASSES, 2, P], F32, name="turn_bank")
            for g in range(PASSES):
                for u in range(2):
                    every_second = words[:, WORDS_PASS * g + u : WORDS_PASS * (g + 1) : 2]
                    nc.tensor.transpose(bank[:, g, u, :], every_second, identity[:])
            target = x_grouped[b][:, :, tt * P * PACK : (tt + 1) * P * PACK].bitcast(F32)
            nc.scalar.copy(
                out=target.rearrange("p g (n u) -> p g n u", u=2),
                in_=bank[:].rearrange("p g u n -> p g n u"),
            )

        def quantize_x_half(b, g, half):
            nc.vector.quantize_mx(
                out=x_codes[b][:, g, half * HALF : (half + 1) * HALF].bitcast(E5M2),
                scales=x_scales[b][:, g, half * HALF : (half + 1) * HALF],
                in_=x_grouped[b][:, g, half * HALF * PACK : (half + 1) * HALF * PACK],
            )

        def quantize_x(b):
            nc.vector.quantize_mx(
                out=x_codes[b][:].rearrange("p g n -> p (g n)").bitcast(E5M2),
                scales=x_scales[b][:].rearrange("p g n -> p (g n)"),
                in_=x_grouped[b][:].rearrange("p g n -> p (g n)"),
            )

        def interleave_w(slab, g, copy):
            phase, proj = divmod(slab, PROJ)
            if phase not in w_grouped:
                columns = PROJ * PASSES * SLAB
                w_grouped[phase] = work.tile([P, PROJ * PASSES, SLAB * PACK], BF16, name="w_grouped", align_bytes=64)
                w_codes[phase] = keep.tile([P, columns], U32, name="w_codes_%d" % phase, align_bytes=64)
                w_scales[phase] = keep.tile([P, columns], U8, name="w_scales_%d" % phase, align_bytes=64)
            copy(
                out=w_grouped[phase][:, proj * PASSES + g, :].rearrange("p (h c i r) -> p h c r i", h=2, i=4, r=PACK),
                in_=w_raw[slab, g][:].rearrange("p r (c i h) -> p h c r i", h=2, i=4),
            )

        def quantize_w(slab):
            phase, proj = divmod(slab, PROJ)
            first, end = proj * PASSES, (proj + 1) * PASSES
            nc.vector.quantize_mx(
                out=w_codes[phase][:, first * SLAB : end * SLAB].bitcast(E4M3),
                scales=w_scales[phase][:, first * SLAB : end * SLAB],
                in_=w_grouped[phase][:, first:end, :].rearrange("p g n -> p (g n)"),
            )

        def count_turns(phase):
            whole[phase] = work.tile([P, T], I32, name="whole_turns")
            nc.vector.tensor_scalar(
                out=whole[phase][:], in0=position[:], scalar1=rate[:, pair_tile(phase), 0:1], scalar2=None, op0=ALU.mult
            )

        def reduce_turns(phase):
            turns[phase] = keep.tile([P, T], F32, name="turns_%d" % phase)
            nc.vector.scalar_tensor_tensor(
                out=turns[phase][:],
                in0=position[:],
                scalar=rate[:, pair_tile(phase), 0:1],
                in1=whole[phase][:],
                op0=ALU.mult,
                op1=ALU.subtract,
            )

        def make_cos(phase):
            forward = rate[:, pair_tile(phase), 0:1]
            tables[phase] = work.tile([P, 3, T], F32, name="table", bufs=3)
            cos = tables[phase][:, 1, :]
            if largest_angle(phase) < math.pi / 2:
                nc.scalar.activation(out=cos, in_=position[:], func=ACT.Sin, scale=forward, bias=math.pi / 2)
                return
            magnitude = work.tile([P, T], F32, name="magnitude")
            if largest_angle(phase) < TWO_PI:
                nc.scalar.activation(out=magnitude[:], in_=position[:], func=ACT.Abs, scale=forward, bias=-math.pi)
                nc.scalar.activation(out=cos, in_=magnitude[:], func=ACT.Sin, bias=-math.pi / 2)
            else:
                nc.scalar.activation(out=magnitude[:], in_=turns[phase][:], func=ACT.Abs)
                nc.scalar.activation(out=cos, in_=magnitude[:], func=ACT.Sin, scale=-TWO_PI, bias=math.pi / 2)

        def make_sin(phase):
            forward, backward = rate[:, pair_tile(phase), 0:1], rate[:, pair_tile(phase), 1:2]
            plus, minus = tables[phase][:, 2, :], tables[phase][:, 0, :]
            if largest_angle(phase) < math.pi / 2:
                nc.scalar.activation(out=plus, in_=position[:], func=ACT.Sin, scale=forward)
                nc.scalar.activation(out=minus, in_=position[:], func=ACT.Sin, scale=backward)
            elif largest_angle(phase) < TWO_PI:
                nc.scalar.activation(out=plus, in_=position[:], func=ACT.Sin, scale=backward, bias=math.pi)
                nc.scalar.activation(out=minus, in_=position[:], func=ACT.Sin, scale=forward, bias=-math.pi)
            else:
                nc.scalar.activation(out=plus, in_=turns[phase][:], func=ACT.Sin, scale=TWO_PI)
                nc.scalar.activation(out=minus, in_=turns[phase][:], func=ACT.Sin, scale=-TWO_PI)

        def multiply(u):
            phase, proj, b = unit_coords(u)
            for h in range(2):
                banks[u, h] = psum.tile([P, T], F32, name="mx_bank")
                for g in range(PASSES):
                    block = 2 * (proj * PASSES + g) + h
                    cols = slice(block * P, (block + 1) * P)
                    nc.tensor.matmul_mx(
                        out=banks[u, h][:],
                        lhsT=w_codes[phase][:, cols].bitcast(E4M3),
                        lhsT_scale=w_scales[phase][:, cols],
                        rhs=x_codes[b][:, g, :].bitcast(E5M2),
                        rhs_scale=x_scales[b][:, g, :],
                        start=(g == 0),
                        stop=(g == PASSES - 1),
                    )

        def rotate(u, h, first, count):
            phase, proj, b = unit_coords(u)
            if first == 0:
                products[u, h] = work.tile([P, 2, T], F32, name="product", bufs=8)
            cols = slice(first, first + count)
            nc.vector.scalar_tensor_tensor(
                out=products[u, h][:, :, cols],
                in0=banks[u, h][:, cols].unsqueeze(1).to_broadcast([P, 2, count]),
                scalar=bias_sb[:, proj, pair_tile(phase), h : h + 1],
                in1=tables[phase][:, 1 - h : 3 - h, cols],
                op0=ALU.add,
                op1=ALU.mult,
            )

        def add_products(u):
            sums[u] = work.tile([P, 2, T], F32, name="total", bufs=3)
            cols = slice(halves_on_tensor(u) * HALF, T)
            nc.gpsimd.tensor_tensor(
                out=sums[u][:, :, cols], in0=products[u, 0][:, :, cols], in1=products[u, 1][:, :, cols], op=ALU.add
            )

        def turn_back(u, half, staged, copy):
            terms = [products[u, 0], products[u, 1]] if half < halves_on_tensor(u) else [sums[u]]
            bank = psum.tile([P, 2, 2, P], F32, name="turn_bank")
            for k in range(2):
                tt = 2 * half + k
                for h in range(2):
                    for i, term in enumerate(terms):
                        nc.tensor.matmul(
                            out=bank[:, k, h, :],
                            lhsT=term[:, h, tt * P : (tt + 1) * P],
                            rhs=identity[:],
                            is_transpose=True,
                            start=(i == 0),
                            stop=(i == len(terms) - 1),
                        )
            copy(
                out=staged[:, 2 * half : 2 * half + 2, :].rearrange("p t (i h) -> p t i h", h=2),
                in_=bank[:].rearrange("p t h i -> p t i h"),
            )

        def store(u, staged, tiles):
            phase, proj, b = unit_coords(u)
            j = pair_tile(phase)
            rows = outs[proj][b, :, j * SLAB : (j + 1) * SLAB].rearrange("(t p) c -> p t c", p=P)
            nc.sync.dma_start(out=rows[:, tiles, :], in_=staged[:, tiles, :])

        def new_staging():
            staged = work.tile([P, TOKEN_TILES, SLAB], F32, name="staged", bufs=6)
            return staged

        def finish(u):
            by_halves = u >= UNITS - HALF_STORES
            staged = new_staging()
            for half in range(2):
                turn_back(u, half, staged, nc.scalar.copy)
                if by_halves:
                    store(u, staged, slice(2 * half, 2 * half + 2))
            if not by_halves:
                store(u, staged, slice(0, TOKEN_TILES))

        bias_rows = keep.tile([P, SLAB], BF16)
        nc.vector.memset(bias_rows[:], 0.0)
        for proj in range(PROJ):
            nc.scalar.dma_start(
                out=bias_rows[proj * PAIR_TILES : (proj + 1) * PAIR_TILES, :],
                in_=biases[proj].rearrange("(j c) -> j c", j=PAIR_TILES),
            )
        load_x(0, 0)
        load_w(0, 0)
        for tt in range(1, TOKEN_TILES):
            load_x(0, tt)
        load_w(0, 1)
        for u in range(1, LOAD_LEAD):
            load_operands(u)

        index = keep.tile([P, PARTITION_BITS], I32)
        nc.gpsimd.iota(index[:], pattern=[[0, PARTITION_BITS]], base=0, channel_multiplier=1)
        shift = keep.tile([P, PARTITION_BITS], I32)
        nc.gpsimd.iota(shift[:], pattern=[[1, PARTITION_BITS]], base=0, channel_multiplier=0)
        identity = keep.tile([P, P], F32)
        make_identity(nc, identity[:])
        position = keep.tile([P, T], F32)
        nc.gpsimd.iota(
            position[:], pattern=[[1, T]], base=0, channel_multiplier=0, allow_small_or_imprecise_dtypes=True
        )

        shifted = keep.tile([P, PARTITION_BITS], I32)
        nc.vector.tensor_tensor(out=shifted[:], in0=index[:], in1=shift[:], op=ALU.logical_shift_right)
        bits = keep.tile([P, PARTITION_BITS], I32)
        nc.vector.tensor_scalar(out=bits[:], in0=shifted[:], scalar1=1, scalar2=None, op0=ALU.bitwise_and)
        factors = keep.tile([P, PARTITION_BITS], F32)
        for bit in range(PARTITION_BITS):
            nc.vector.tensor_scalar(
                out=factors[:, bit : bit + 1],
                in0=bits[:, bit : bit + 1],
                scalar1=THETA ** (-(2**bit) / PAIRS) - 1.0,
                scalar2=1.0,
                op0=ALU.mult,
                op1=ALU.add,
            )
        base_rate = keep.tile([P, 1], F32)
        nc.vector.tensor_reduce(out=base_rate[:], in_=factors[:], axis=mybir.AxisListType.X, op=ALU.mult)
        rate = keep.tile([P, PAIR_TILES, 2], F32)
        reduced = [phase for phase in range(PAIR_TILES) if largest_angle(phase) >= TWO_PI]
        for phase in range(PAIR_TILES):
            radians = first_rate(phase)
            for i, scale in enumerate((radians / TWO_PI,) if phase in reduced else (radians, -radians)):
                nc.vector.tensor_scalar(
                    out=rate[:, pair_tile(phase), i : i + 1], in0=base_rate[:], scalar1=scale, scalar2=None, op0=ALU.mult
                )

        make_cos(0)
        make_sin(0)
        for phase in reduced:
            count_turns(phase)
        for phase in reduced:
            reduce_turns(phase)

        for tt in range(TOKEN_TILES):
            transpose_x(0, tt)
        bias_bank = psum.tile([P, PASSES, 2, P], F32, name="turn_bank")
        nc.tensor.transpose(bias_bank[:, 0, 0, :], bias_rows[:].bitcast(F32), identity[:])
        bias_sb = keep.tile([P, PROJ, PAIR_TILES, 2], BF16)
        nc.scalar.copy(out=bias_sb[:].rearrange("p a j h -> p (a j h)").bitcast(F32), in_=bias_bank[:, 0, 0, 0:SLABS])
        for g in range(PASSES):
            interleave_w(0, g, nc.vector.tensor_copy)
            quantize_x_half(0, g, 0)
        quantize_w(0)
        for g in range(PASSES):
            quantize_x_half(0, g, 1)
        interleave_w(1, 0, nc.vector.tensor_copy)
        interleave_w(1, 1, nc.scalar.copy)
        transpose_x(1, 0)
        multiply(0)
        quantize_w(1)
        make_cos(1)
        for tt in range(1, TOKEN_TILES):
            transpose_x(1, tt)

        finished = 0
        for step in range(UNITS - 1):
            multiply(step + 1)
            if step == 0:
                make_sin(1)
            for at in slab_at:
                for g in range(PASSES):
                    if step == max(at - W_LEAD + g, 0):
                        interleave_w(slab_at[at], g, nc.scalar.copy)
            for phase in reduced:
                if step == first_of_slab[PROJ * phase] - TABLE_LEAD:
                    make_cos(phase)
                if step == first_of_slab[PROJ * phase] - TABLE_LEAD + 1:
                    make_sin(phase)
            rotate(step, 0, 0, T)
            for b in range(2, B):
                tt = step - (first_of_batch[b] - X_LEAD)
                if 0 <= tt < TOKEN_TILES:
                    transpose_x(b, tt)
            rotate(step, 1, 0, T)
            if step in batch_at:
                quantize_x(batch_at[step])
            if step in slab_at:
                quantize_w(slab_at[step])
            if halves_on_tensor(step) < 2:
                add_products(step)
            while finished <= step - (FINISH_LAG if finished < UNITS - TAIL else FINISH_LAG - 1):
                finish(finished)
                finished += 1
            load_operands(step + LOAD_LEAD)

        last = UNITS - 1
        staged = new_staging()
        for h in range(2):
            rotate(last, h, 0, HALF)
        finish(last - 1)
        for h in range(2):
            rotate(last, h, HALF, HALF)
        for half, copy in enumerate((nc.vector.tensor_copy, nc.scalar.copy)):
            turn_back(last, half, staged, copy)
            store(last, staged, slice(2 * half, 2 * half + 2))
